import numpy as np
import ml_dtypes


def mxq(x, axis, fmt="e4m3"):
    dtype, down = {"e4m3": (ml_dtypes.float8_e4m3fn, 7), "e5m2": (ml_dtypes.float8_e5m2, 14)}[fmt]
    v = np.moveaxis(np.asarray(x, np.float32).astype(ml_dtypes.bfloat16).astype(np.float64), axis, -1)
    blocks = v.reshape(v.shape[:-1] + (-1, 32))
    amax = np.abs(blocks).max(-1, keepdims=True)
    byte = np.maximum(np.where(amax > 0, np.frexp(amax)[1] - 1 + 127, 0) - down, 1)
    scale = np.exp2(byte - 127.0)
    codes = (blocks / scale).astype(np.float32).astype(dtype).astype(np.float64)
    return np.moveaxis((codes * scale).reshape(v.shape), -1, axis)


WIDE = False


def mx_kscale(k):
    if not WIDE:
        return np.ones(k)
    levels = np.array([10, -10, 5, -5, 0])
    if k % 512:
        return np.exp2(np.random.permutation(np.resize(levels, k // 32))).repeat(32)
    a = np.empty((k // 512, 16))
    for p in range(k // 512):
        a[p, :8] = np.random.permutation(np.resize(levels, 8))
        for g in range(8):
            far = levels[np.abs(levels - a[p, g]) >= 10]
            a[p, g + 8] = far[np.random.randint(len(far))]
    return np.exp2(a.ravel()).repeat(32)


BF16 = ml_dtypes.bfloat16


def bf(x):
    return np.asarray(x, np.float32).astype(BF16)


def f64(x):
    return np.asarray(x).astype(np.float64)


B, CIN, COUT, E, G, NC = 8192, 512, 256, 4, 2, 2
OMEGA_0 = 30.0


def setup_inputs():
    s = mx_kscale(CIN)
    wb = np.sqrt(6.0 / CIN) / OMEGA_0
    return {"in_feats": bf(np.random.standard_normal((B, CIN)) * s),
            "tile_gate": bf(np.random.standard_normal((B, E)) / np.sqrt(E)),
            "W": bf(np.random.uniform(-wb, wb, (E, COUT, CIN)) / s)}


def reference(in_feats, tile_gate, W):
    xq = mxq(f64(in_feats), 1, "e4m3")
    wq = mxq(f64(W), 2, "e4m3")
    g = f64(tile_gate)
    out = np.zeros((B, COUT))
    for t in range(E):
        out = out + g[:, t:t + 1] * (xq @ wq[t].T)
    return np.sin(OMEGA_0 * out)

@@ -1,0 +1,235 @@
+import math
+from contextlib import ExitStack
+
+import concourse.mybir as mybir
+from concourse.masks import make_identity
+
+F32 = mybir.dt.float32
+BF16 = mybir.dt.bfloat16
+I32 = mybir.dt.int32
+U32 = mybir.dt.uint32
+U8 = mybir.dt.uint8
+FP8X4 = mybir.dt.float8_e4m3fn_x4
+ALU = mybir.AluOpType
+ACT = mybir.ActivationFunctionType
+
+P = 128
+B, CIN, COUT, E = 8192, 512, 256, 4
+NT = B // P
+GT = 4
+NG = NT // GT
+FLOPS = 2 * B * CIN * COUT * E
+
+MANUAL = False
+TWO = (False, True, False, True)
+EXIT_ENG = ("s", "s")
+CAST_ENG = "g"
+LEAD_T = 2
+LEAD_Q = 1
+
+
+def tile_sinelayer_loe_pa_t_kernel(tc, in_feats, tile_gate, W, out):
+    nc = tc.nc
+    x_v = in_feats.rearrange("(p r) k -> p (r k)", p=P)
+    g_v = tile_gate.rearrange("(p r) e -> p (r e)", p=P)
+    w_v = W.rearrange("t (h p) k -> p (t h) k", p=P)
+    o_v = out.rearrange("(p r) c -> p (r c)", p=P)
+
+    with ExitStack() as ctx:
+        if MANUAL:
+            ctx.enter_context(tc.manual_schedule())
+        const = ctx.enter_context(tc.tile_pool(name="const", bufs=1))
+        gpool = ctx.enter_context(tc.tile_pool(name="gpool", bufs=LEAD_T + 2))
+        spool = ctx.enter_context(tc.tile_pool(name="spool", bufs=4))
+        rpool = ctx.enter_context(tc.tile_pool(name="rpool", bufs=3))
+        psx = ctx.enter_context(tc.psum_pool(name="psx", bufs=2))
+        psp = ctx.enter_context(tc.psum_pool(name="psp", bufs=3))
+
+        w_sb = const.tile([P, 8 * CIN], BF16, name="w_sb")
+        w_sb3 = w_sb[:].rearrange("p (a k) -> p a k", a=8)
+        def load_w(q):
+            nc.sync.dma_start(out=w_sb3[:, 2 * q:2 * q + 2, :], in_=w_v[:, 2 * q:2 * q + 2, :])
+
+        gate_sb = const.tile([P, NT * E], BF16, name="gate_sb")
+        nc.scalar.dma_start(out=gate_sb[:], in_=g_v)
+        xs = []
+        for g in range(NG):
+            x_t = const.tile([P, GT * CIN], BF16, name="x%d" % g)
+            xs.append(x_t)
+        half = GT * CIN // 2
+        load_w(0)
+        load_w(1)
+        nc.sync.dma_start(out=xs[0][:, 0:half], in_=x_v[:, 0:half])
+        load_w(2)
+        load_w(3)
+        nc.sync.dma_start(out=xs[0][:, half:2 * half], in_=x_v[:, half:2 * half])
+        for g in range(1, NG):
+            nc.sync.dma_start(out=xs[g][:], in_=x_v[:, g * GT * CIN:(g + 1) * GT * CIN])
+
+        ident = const.tile([P, P], F32, name="ident")
+        make_identity(nc, ident[:])
+        zero = const.tile([P, 1], F32, name="zero")
+        nc.vector.memset(zero[:], 0.0)
+        warm = const.tile([P, 1], F32, name="warm")
+        nc.scalar.activation(out=warm[:], in_=zero[:], func=ACT.Sin)
+        gs = const.tile([P, NT * E], F32, name="gs")
+        nc.vector.tensor_scalar(out=gs[:], in0=gate_sb[:], scalar1=30.0 / (2.0 * math.pi),
+                                scalar2=None, op0=ALU.mult)
+
+        def copy_out(eng, dst, src):
+            if eng == "s":
+                nc.scalar.copy(out=dst, in_=src)
+            else:
+                nc.vector.tensor_copy(out=dst, in_=src)
+
+        def transposes(bank, src_f32, first):
+            for jj in range(2):
+                for u in range(2):
+                    c = (first + jj) * 256
+                    nc.tensor.transpose(bank[:, (jj * 2 + u) * P:(jj * 2 + u + 1) * P],
+                                        src_f32[:, c + u:c + 256:2], ident[:])
+
+        def regroup(eng, grp_f32, h, bank):
+            copy_out(eng,
+                     grp_f32[:, h * 512:(h + 1) * 512].rearrange("p (j m u) -> p j m u", j=2, u=2),
+                     bank[:].rearrange("p (j u m) -> p j m u", j=2, u=2))
+
+        w_f32 = w_sb[:].bitcast(F32)
+        w_grp = const.tile([P, 8 * CIN], BF16, name="w_grp", align_bytes=64)
+        w_grp_f32 = w_grp[:].bitcast(F32)
+        w_codes = const.tile([P, E * COUT], U32, name="w_codes", align_bytes=64)
+        w_scl = const.tile([P, E * COUT], U8, name="w_scl", align_bytes=64)
+        for q in range(4):
+            wt = psp.tile([P, 512], F32, tag=("pa" if q % 2 == 0 else "pb"), name="wt%d" % q)
+            transposes(wt, w_f32, 2 * q)
+            regroup("s" if q % 2 == 0 else "v", w_grp_f32, q, wt)
+            if q % 2 == 1:
+                h = q // 2
+                nc.vector.quantize_mx(out=w_codes[:, h * 512:(h + 1) * 512].bitcast(FP8X4),
+                                      scales=w_scl[:, h * 512:(h + 1) * 512],
+                                      in_=w_grp[:, h * 2048:(h + 1) * 2048])
+
+        grp = {}
+        banks = {}
+        codes = {}
+        scl = {}
+        u_t = {}
+        o_t = {}
+        k_t = {}
+        r_t = {}
+
+        def stage_t(g):
+            grp[g] = gpool.tile([P, GT * CIN], BF16, tag="grp", name="grp%d" % g, align_bytes=64)
+            xf = xs[g][:].bitcast(F32)
+            for h in range(2):
+                bank = psx.tile([P, 512], F32, tag="xt", name="xt%d_%d" % (g, h))
+                transposes(bank, xf, 2 * h)
+                banks[(g, h)] = bank
+
+        def stage_exit(g, h):
+            regroup(EXIT_ENG[h], grp[g][:].bitcast(F32), h, banks[(g, h)])
+
+        def stage_q(g):
+            codes[g] = gpool.tile([P, GT * P], U32, tag="codes", name="codes%d" % g, align_bytes=64)
+            scl[g] = gpool.tile([P, GT * P], U8, tag="scl", name="scl%d" % g, align_bytes=64)
+            cuts = ((0, 2), (2, 4)) if g == 0 else ((0, 4),)
+            for lo, hi in cuts:
+                nc.vector.quantize_mx(out=codes[g][:, lo * P:hi * P].bitcast(FP8X4),
+                                      scales=scl[g][:, lo * P:hi * P],
+                                      in_=grp[g][:, lo * CIN:hi * CIN])
+
+        def stage_m(g, jj):
+            if jj == 0:
+                u_t[g] = rpool.tile([P, GT * COUT], F32, tag="u", name="u%d" % g)
+            j = g * GT + jj
+            pa = psp.tile([P, 512], F32, tag="pa", name="pa%d" % j)
+            pb = psp.tile([P, 512], F32, tag="pb", name="pb%d" % j)
+            for h, bank in ((0, pa), (1, pb)):
+                nc.tensor.matmul_mx(out=bank[:],
+                                    lhsT=codes[g][:, jj * P:(jj + 1) * P].bitcast(FP8X4),
+                                    lhsT_scale=scl[g][:, jj * P:(jj + 1) * P],
+                                    rhs=w_codes[:, h * 512:(h + 1) * 512].bitcast(FP8X4),
+                                    rhs_scale=w_scl[:, h * 512:(h + 1) * 512],
+                                    start=True, stop=True)
+
+            def gcol(t):
+                return gs[:, j * E + t:j * E + t + 1]
+
+            def stt(dst, src, t, add):
+                nc.vector.scalar_tensor_tensor(out=dst, in0=src, scalar=gcol(t), in1=add,
+                                               op0=ALU.mult, op1=ALU.add)
+
+            u_dst = u_t[g][:, jj * COUT:(jj + 1) * COUT]
+            sa0 = spool.tile([P, COUT], F32, tag="sa0", name="sa0_%d" % j)
+            nc.scalar.activation(out=sa0[:], in_=pa[:, 0:COUT], func=ACT.Copy, scale=gcol(0))
+            acc = spool.tile([P, COUT], F32, tag="acc", name="acc%d" % j)
+            if TWO[jj]:
+                sa1 = spool.tile([P, COUT], F32, tag="sa1", name="sa1_%d" % j)
+                nc.scalar.activation(out=sa1[:], in_=pa[:, COUT:2 * COUT], func=ACT.Copy, scale=gcol(1))
+                a01 = spool.tile([P, COUT], F32, tag="a01", name="a01_%d" % j)
+                nc.gpsimd.tensor_tensor(out=a01[:], in0=sa0[:], in1=sa1[:], op=ALU.add)
+                stt(acc[:], pb[:, 0:COUT], 2, a01[:])
+            else:
+                acc1 = spool.tile([P, COUT], F32, tag="acc1", name="acc1_%d" % j)
+                stt(acc1[:], pa[:, COUT:2 * COUT], 1, sa0[:])
+                stt(acc[:], pb[:, 0:COUT], 2, acc1[:])
+            stt(u_dst, pb[:, COUT:2 * COUT], 3, acc[:])
+
+        def stage_cast(g, h):
+            k_t[(g, h)] = rpool.tile([P, 512], I32, tag="k", name="k%d_%d" % (g, h))
+            src = u_t[g][:, h * 512:(h + 1) * 512]
+            if CAST_ENG == "g":
+                nc.gpsimd.tensor_scalar(out=k_t[(g, h)][:], in0=src, scalar1=1.0, scalar2=0.0,
+                                        op0=ALU.mult, op1=ALU.add)
+            else:
+                nc.vector.tensor_copy(out=k_t[(g, h)][:], in_=src)
+
+        def stage_sub(g, h):
+            r_t[(g, h)] = rpool.tile([P, 512], F32, tag="r", name="r%d_%d" % (g, h))
+            nc.vector.tensor_tensor(out=r_t[(g, h)][:], in0=u_t[g][:, h * 512:(h + 1) * 512],
+                                    in1=k_t[(g, h)][:], op=ALU.subtract)
+
+        def stage_sin(g, h):
+            if h == 0:
+                o_t[g] = rpool.tile([P, GT * COUT], F32, tag="o", name="o%d" % g)
+            nc.scalar.activation(out=o_t[g][:, h * 512:(h + 1) * 512], in_=r_t[(g, h)][:],
+                                 func=ACT.Sin, scale=2.0 * math.pi)
+            if h == 1:
+                nc.sync.dma_start(out=o_v[:, g * GT * COUT:(g + 1) * GT * COUT], in_=o_t[g][:])
+
+        def tail_piece(g, lo, hi):
+            kk = rpool.tile([P, 256], I32, tag="kk", name="kk%d" % lo)
+            rr = rpool.tile([P, 256], F32, tag="rr", name="rr%d" % lo)
+            oo = rpool.tile([P, 256], F32, tag="oo", name="oo%d" % lo)
+            nc.vector.tensor_copy(out=kk[:], in_=u_t[g][:, lo:hi])
+            nc.vector.tensor_tensor(out=rr[:], in0=u_t[g][:, lo:hi], in1=kk[:], op=ALU.subtract)
+            nc.scalar.activation(out=oo[:], in_=rr[:], func=ACT.Sin, scale=2.0 * math.pi)
+            nc.sync.dma_start(out=o_v[:, g * GT * COUT + lo:g * GT * COUT + hi], in_=oo[:])
+
+        for i in range(-LEAD_T, NG + 1):
+            tg, qg, mg, rg = i + LEAD_T, i + LEAD_Q, i, i - 1
+            has_t = tg < NG
+            has_q = 0 <= qg < NG
+            has_m = 0 <= mg < NG
+            has_r = 0 <= rg < NG - 1
+            if has_t:
+                stage_t(tg)
+            for s in range(GT):
+                if has_r and s == 0:
+                    stage_cast(rg, 0)
+                if has_m:
+                    stage_m(mg, s)
+                    if mg == NG - 1:
+                        tail_piece(mg, s * COUT, (s + 1) * COUT)
+                if has_r and s == 1:
+                    stage_cast(rg, 1)
+                if has_r and s == 0:
+                    stage_sub(rg, 0)
+                if has_q and s == 1:
+                    stage_q(qg)
+                if has_r and s == 2:
+                    stage_sub(rg, 1)
+                if has_t and s < 2:
+                    stage_exit(tg, s)
+                if has_r and s >= 2:
+                    stage_sin(rg, s - 2)

@@ -18,14 +18,8 @@ B, CIN, COUT, E = 8192, 512, 256, 4
 NT = B // P
 GT = 4
 NG = NT // GT
+GW = GT * COUT
 FLOPS = 2 * B * CIN * COUT * E
-
-MANUAL = False
-TWO = (False, True, False, True)
-EXIT_ENG = ("s", "s")
-CAST_ENG = "g"
-LEAD_T = 2
-LEAD_Q = 1
 
 
 def tile_sinelayer_loe_pa_t_kernel(tc, in_feats, tile_gate, W, out):
@@ -36,17 +30,17 @@ def tile_sinelayer_loe_pa_t_kernel(tc, in_feats, tile_gate, W, out):
     o_v = out.rearrange("(p r) c -> p (r c)", p=P)
 
     with ExitStack() as ctx:
-        if MANUAL:
-            ctx.enter_context(tc.manual_schedule())
+        ctx.enter_context(tc.manual_schedule())
         const = ctx.enter_context(tc.tile_pool(name="const", bufs=1))
-        gpool = ctx.enter_context(tc.tile_pool(name="gpool", bufs=LEAD_T + 2))
-        spool = ctx.enter_context(tc.tile_pool(name="spool", bufs=4))
+        gpool = ctx.enter_context(tc.tile_pool(name="gpool", bufs=4))
+        spool = ctx.enter_context(tc.tile_pool(name="spool", bufs=5))
         rpool = ctx.enter_context(tc.tile_pool(name="rpool", bufs=3))
         psx = ctx.enter_context(tc.psum_pool(name="psx", bufs=2))
         psp = ctx.enter_context(tc.psum_pool(name="psp", bufs=3))
 
         w_sb = const.tile([P, 8 * CIN], BF16, name="w_sb")
         w_sb3 = w_sb[:].rearrange("p (a k) -> p a k", a=8)
+
         def load_w(q):
             nc.sync.dma_start(out=w_sb3[:, 2 * q:2 * q + 2, :], in_=w_v[:, 2 * q:2 * q + 2, :])
 
@@ -76,12 +70,6 @@ def tile_sinelayer_loe_pa_t_kernel(tc, in_feats, tile_gate, W, out):
         nc.vector.tensor_scalar(out=gs[:], in0=gate_sb[:], scalar1=30.0 / (2.0 * math.pi),
                                 scalar2=None, op0=ALU.mult)
 
-        def copy_out(eng, dst, src):
-            if eng == "s":
-                nc.scalar.copy(out=dst, in_=src)
-            else:
-                nc.vector.tensor_copy(out=dst, in_=src)
-
         def transposes(bank, src_f32, first):
             for jj in range(2):
                 for u in range(2):
@@ -90,24 +78,23 @@ def tile_sinelayer_loe_pa_t_kernel(tc, in_feats, tile_gate, W, out):
                                         src_f32[:, c + u:c + 256:2], ident[:])
 
         def regroup(eng, grp_f32, h, bank):
-            copy_out(eng,
-                     grp_f32[:, h * 512:(h + 1) * 512].rearrange("p (j m u) -> p j m u", j=2, u=2),
-                     bank[:].rearrange("p (j u m) -> p j m u", j=2, u=2))
+            dst = grp_f32[:, h * 512:(h + 1) * 512].rearrange("p (j m u) -> p j m u", j=2, u=2)
+            src = bank[:].rearrange("p (j u m) -> p j m u", j=2, u=2)
+            if eng == "s":
+                nc.scalar.copy(out=dst, in_=src)
+            else:
+                nc.vector.tensor_copy(out=dst, in_=src)
+
+        def quant(codes, scl, grp, lo, hi):
+            nc.vector.quantize_mx(out=codes[:, lo * P:hi * P].bitcast(FP8X4),
+                                  scales=scl[:, lo * P:hi * P],
+                                  in_=grp[:, lo * CIN:hi * CIN])
 
         w_f32 = w_sb[:].bitcast(F32)
         w_grp = const.tile([P, 8 * CIN], BF16, name="w_grp", align_bytes=64)
         w_grp_f32 = w_grp[:].bitcast(F32)
         w_codes = const.tile([P, E * COUT], U32, name="w_codes", align_bytes=64)
         w_scl = const.tile([P, E * COUT], U8, name="w_scl", align_bytes=64)
-        for q in range(4):
-            wt = psp.tile([P, 512], F32, tag=("pa" if q % 2 == 0 else "pb"), name="wt%d" % q)
-            transposes(wt, w_f32, 2 * q)
-            regroup("s" if q % 2 == 0 else "v", w_grp_f32, q, wt)
-            if q % 2 == 1:
-                h = q // 2
-                nc.vector.quantize_mx(out=w_codes[:, h * 512:(h + 1) * 512].bitcast(FP8X4),
-                                      scales=w_scl[:, h * 512:(h + 1) * 512],
-                                      in_=w_grp[:, h * 2048:(h + 1) * 2048])
 
         grp = {}
         banks = {}
@@ -117,31 +104,31 @@ def tile_sinelayer_loe_pa_t_kernel(tc, in_feats, tile_gate, W, out):
         o_t = {}
         k_t = {}
         r_t = {}
+        prod = {}
 
-        def stage_t(g):
-            grp[g] = gpool.tile([P, GT * CIN], BF16, tag="grp", name="grp%d" % g, align_bytes=64)
-            xf = xs[g][:].bitcast(F32)
-            for h in range(2):
-                bank = psx.tile([P, 512], F32, tag="xt", name="xt%d_%d" % (g, h))
-                transposes(bank, xf, 2 * h)
-                banks[(g, h)] = bank
+        def w_transpose(q):
+            wt = psp.tile([P, 512], F32, tag=("pa" if q % 2 == 0 else "pb"), name="wt%d" % q)
+            transposes(wt, w_f32, 2 * q)
+            return wt
 
-        def stage_exit(g, h):
-            regroup(EXIT_ENG[h], grp[g][:].bitcast(F32), h, banks[(g, h)])
+        def x_transpose(g, h):
+            if h == 0:
+                grp[g] = gpool.tile([P, GT * CIN], BF16, tag="grp", name="grp%d" % g, align_bytes=64)
+            bank = psx.tile([P, 512], F32, tag="xt", name="xt%d_%d" % (g, h))
+            transposes(bank, xs[g][:].bitcast(F32), 2 * h)
+            banks[(g, h)] = bank
 
-        def stage_q(g):
-            codes[g] = gpool.tile([P, GT * P], U32, tag="codes", name="codes%d" % g, align_bytes=64)
-            scl[g] = gpool.tile([P, GT * P], U8, tag="scl", name="scl%d" % g, align_bytes=64)
-            cuts = ((0, 2), (2, 4)) if g == 0 else ((0, 4),)
-            for lo, hi in cuts:
-                nc.vector.quantize_mx(out=codes[g][:, lo * P:hi * P].bitcast(FP8X4),
-                                      scales=scl[g][:, lo * P:hi * P],
-                                      in_=grp[g][:, lo * CIN:hi * CIN])
+        def x_exit(eng, g, h):
+            regroup(eng, grp[g][:].bitcast(F32), h, banks[(g, h)])
 
-        def stage_m(g, jj):
-            if jj == 0:
-                u_t[g] = rpool.tile([P, GT * COUT], F32, tag="u", name="u%d" % g)
-            j = g * GT + jj
+        def x_quant(g, lo, hi):
+            if lo == 0:
+                codes[g] = gpool.tile([P, GT * P], U32, tag="codes", name="codes%d" % g, align_bytes=64)
+                scl[g] = gpool.tile([P, GT * P], U8, tag="scl", name="scl%d" % g, align_bytes=64)
+            quant(codes[g], scl[g], grp[g], lo, hi)
+
+        def mm(j):
+            g, jj = j // GT, j % GT
             pa = psp.tile([P, 512], F32, tag="pa", name="pa%d" % j)
             pb = psp.tile([P, 512], F32, tag="pb", name="pb%d" % j)
             for h, bank in ((0, pa), (1, pb)):
@@ -151,85 +138,128 @@ def tile_sinelayer_loe_pa_t_kernel(tc, in_feats, tile_gate, W, out):
                                     rhs=w_codes[:, h * 512:(h + 1) * 512].bitcast(FP8X4),
                                     rhs_scale=w_scl[:, h * 512:(h + 1) * 512],
                                     start=True, stop=True)
+            prod[j] = (pa, pb)
 
-            def gcol(t):
-                return gs[:, j * E + t:j * E + t + 1]
+        def gcol(j, t):
+            return gs[:, j * E + t:j * E + t + 1]
 
-            def stt(dst, src, t, add):
-                nc.vector.scalar_tensor_tensor(out=dst, in0=src, scalar=gcol(t), in1=add,
+        s_t = {}
+        b_t = {}
+
+        def s_products(j):
+            pa = prod[j][0]
+            for t in range(2):
+                s = spool.tile([P, COUT], F32, tag="s%d" % t, name="s%d_%d" % (t, j))
+                nc.scalar.activation(out=s[:], in_=pa[:, t * COUT:(t + 1) * COUT], func=ACT.Copy,
+                                     scale=gcol(j, t))
+                s_t[(j, t)] = s
+
+        def v_products(j):
+            pb = prod[j][1]
+            for t in range(2):
+                b = spool.tile([P, COUT], F32, tag="b%d" % t, name="b%d_%d" % (t, j))
+                nc.vector.scalar_tensor_tensor(out=b[:], in0=pb[:, t * COUT:(t + 1) * COUT],
+                                               scalar=gcol(j, 2 + t), in1=s_t[(j, t)][:],
                                                op0=ALU.mult, op1=ALU.add)
+                b_t[(j, t)] = b
 
-            u_dst = u_t[g][:, jj * COUT:(jj + 1) * COUT]
-            sa0 = spool.tile([P, COUT], F32, tag="sa0", name="sa0_%d" % j)
-            nc.scalar.activation(out=sa0[:], in_=pa[:, 0:COUT], func=ACT.Copy, scale=gcol(0))
-            acc = spool.tile([P, COUT], F32, tag="acc", name="acc%d" % j)
-            if TWO[jj]:
-                sa1 = spool.tile([P, COUT], F32, tag="sa1", name="sa1_%d" % j)
-                nc.scalar.activation(out=sa1[:], in_=pa[:, COUT:2 * COUT], func=ACT.Copy, scale=gcol(1))
-                a01 = spool.tile([P, COUT], F32, tag="a01", name="a01_%d" % j)
-                nc.gpsimd.tensor_tensor(out=a01[:], in0=sa0[:], in1=sa1[:], op=ALU.add)
-                stt(acc[:], pb[:, 0:COUT], 2, a01[:])
-            else:
-                acc1 = spool.tile([P, COUT], F32, tag="acc1", name="acc1_%d" % j)
-                stt(acc1[:], pa[:, COUT:2 * COUT], 1, sa0[:])
-                stt(acc[:], pb[:, 0:COUT], 2, acc1[:])
-            stt(u_dst, pb[:, COUT:2 * COUT], 3, acc[:])
+        def add(eng, j):
+            g, jj = j // GT, j % GT
+            if jj == 0:
+                u_t[g] = rpool.tile([P, GW], F32, tag="u", name="u%d" % g)
+            e = nc.gpsimd if eng == "g" else nc.vector
+            e.tensor_tensor(out=u_t[g][:, jj * COUT:(jj + 1) * COUT], in0=b_t[(j, 0)][:],
+                            in1=b_t[(j, 1)][:], op=ALU.add)
 
-        def stage_cast(g, h):
-            k_t[(g, h)] = rpool.tile([P, 512], I32, tag="k", name="k%d_%d" % (g, h))
-            src = u_t[g][:, h * 512:(h + 1) * 512]
-            if CAST_ENG == "g":
-                nc.gpsimd.tensor_scalar(out=k_t[(g, h)][:], in0=src, scalar1=1.0, scalar2=0.0,
-                                        op0=ALU.mult, op1=ALU.add)
-            else:
-                nc.vector.tensor_copy(out=k_t[(g, h)][:], in_=src)
+        def cast(g, lo, hi):
+            if lo == 0:
+                k_t[g] = rpool.tile([P, GW], I32, tag="k", name="k%d" % g)
+                r_t[g] = rpool.tile([P, GW], F32, tag="r", name="r%d" % g)
+                o_t[g] = rpool.tile([P, GW], F32, tag="o", name="o%d" % g)
+            nc.vector.tensor_copy(out=k_t[g][:, lo:hi], in_=u_t[g][:, lo:hi])
 
-        def stage_sub(g, h):
-            r_t[(g, h)] = rpool.tile([P, 512], F32, tag="r", name="r%d_%d" % (g, h))
-            nc.vector.tensor_tensor(out=r_t[(g, h)][:], in0=u_t[g][:, h * 512:(h + 1) * 512],
-                                    in1=k_t[(g, h)][:], op=ALU.subtract)
+        def sub(g, lo, hi):
+            nc.vector.tensor_tensor(out=r_t[g][:, lo:hi], in0=u_t[g][:, lo:hi],
+                                    in1=k_t[g][:, lo:hi], op=ALU.subtract)
 
-        def stage_sin(g, h):
-            if h == 0:
-                o_t[g] = rpool.tile([P, GT * COUT], F32, tag="o", name="o%d" % g)
-            nc.scalar.activation(out=o_t[g][:, h * 512:(h + 1) * 512], in_=r_t[(g, h)][:],
-                                 func=ACT.Sin, scale=2.0 * math.pi)
-            if h == 1:
-                nc.sync.dma_start(out=o_v[:, g * GT * COUT:(g + 1) * GT * COUT], in_=o_t[g][:])
+        def sine(g, lo, hi):
+            nc.scalar.activation(out=o_t[g][:, lo:hi], in_=r_t[g][:, lo:hi], func=ACT.Sin,
+                                 scale=2.0 * math.pi)
 
-        def tail_piece(g, lo, hi):
-            kk = rpool.tile([P, 256], I32, tag="kk", name="kk%d" % lo)
-            rr = rpool.tile([P, 256], F32, tag="rr", name="rr%d" % lo)
-            oo = rpool.tile([P, 256], F32, tag="oo", name="oo%d" % lo)
-            nc.vector.tensor_copy(out=kk[:], in_=u_t[g][:, lo:hi])
-            nc.vector.tensor_tensor(out=rr[:], in0=u_t[g][:, lo:hi], in1=kk[:], op=ALU.subtract)
-            nc.scalar.activation(out=oo[:], in_=rr[:], func=ACT.Sin, scale=2.0 * math.pi)
-            nc.sync.dma_start(out=o_v[:, g * GT * COUT + lo:g * GT * COUT + hi], in_=oo[:])
+        def store(g, lo, hi):
+            nc.sync.dma_start(out=o_v[:, g * GW + lo:g * GW + hi], in_=o_t[g][:, lo:hi])
 
-        for i in range(-LEAD_T, NG + 1):
-            tg, qg, mg, rg = i + LEAD_T, i + LEAD_Q, i, i - 1
-            has_t = tg < NG
-            has_q = 0 <= qg < NG
-            has_m = 0 <= mg < NG
-            has_r = 0 <= rg < NG - 1
-            if has_t:
-                stage_t(tg)
+        wt0 = w_transpose(0)
+        regroup("s", w_grp_f32, 0, wt0)
+        wt1 = w_transpose(1)
+        regroup("v", w_grp_f32, 1, wt1)
+        quant(w_codes, w_scl, w_grp, 0, 4)
+        x_transpose(0, 0)
+        x_exit("s", 0, 0)
+        x_quant(0, 0, 2)
+        wt2 = w_transpose(2)
+        regroup("s", w_grp_f32, 2, wt2)
+        wt3 = w_transpose(3)
+        regroup("v", w_grp_f32, 3, wt3)
+        quant(w_codes, w_scl, w_grp, 4, 8)
+        x_transpose(0, 1)
+        x_exit("s", 0, 1)
+        x_quant(0, 2, 4)
+        for h in range(2):
+            x_transpose(1, h)
+            x_exit("s", 1, h)
+
+        H = GW // 2
+        for g in range(NG):
+            last = g == NG - 1
             for s in range(GT):
-                if has_r and s == 0:
-                    stage_cast(rg, 0)
-                if has_m:
-                    stage_m(mg, s)
-                    if mg == NG - 1:
-                        tail_piece(mg, s * COUT, (s + 1) * COUT)
-                if has_r and s == 1:
-                    stage_cast(rg, 1)
-                if has_r and s == 0:
-                    stage_sub(rg, 0)
-                if has_q and s == 1:
-                    stage_q(qg)
-                if has_r and s == 2:
-                    stage_sub(rg, 1)
-                if has_t and s < 2:
-                    stage_exit(tg, s)
-                if has_r and s >= 2:
-                    stage_sin(rg, s - 2)
+                j = g * GT + s
+                if s % 2 == 0:
+                    if g + 2 < NG:
+                        x_transpose(g + 2, s // 2)
+                    mm(j)
+                    mm(j + 1)
+                s_products(j)
+                if not last:
+                    if s % 2 == 1 and g + 2 < NG:
+                        x_exit("s", g + 2, s // 2)
+                    if s % 2 == 0 and g >= 2:
+                        sine(g - 2, (s // 2) * H, (s // 2 + 1) * H)
+                        if s == 2:
+                            store(g - 2, 0, GW)
+                else:
+                    if s < 2:
+                        sine(g - 2, s * H, (s + 1) * H)
+                        if s == 1:
+                            store(g - 2, 0, GW)
+                    if s == 3:
+                        sine(g - 1, 0, H)
+                v_products(j)
+                if not (last and s == 3):
+                    add("g", j)
+                if not last:
+                    if s == 0:
+                        x_quant(g + 1, 0, GT)
+                    elif g >= 1:
+                        if s == 1:
+                            cast(g - 1, 0, GW)
+                        else:
+                            sub(g - 1, (s - 2) * H, (s - 1) * H)
+                else:
+                    if s == 0:
+                        cast(g - 1, 0, GW)
+                    elif s < 3:
+                        sub(g - 1, (s - 1) * H, s * H)
+                    else:
+                        cast(g, 0, 2 * COUT)
+                        add("v", j)
+                        sub(g, 0, 2 * COUT)
+                        cast(g, 2 * COUT, 4 * COUT)
+                        sine(g - 1, H, GW)
+                        store(g - 1, 0, GW)
+                        sine(g, 0, 2 * COUT)
+                        store(g, 0, 2 * COUT)
+                        for q in range(2, GT):
+                            sub(g, q * COUT, (q + 1) * COUT)
+                            sine(g, q * COUT, (q + 1) * COUT)
+                            store(g, q * COUT, (q + 1) * COUT)

@@ -127,18 +127,17 @@ def tile_sinelayer_loe_pa_t_kernel(tc, in_feats, tile_gate, W, out):
                 scl[g] = gpool.tile([P, GT * P], U8, tag="scl", name="scl%d" % g, align_bytes=64)
             quant(codes[g], scl[g], grp[g], lo, hi)
 
-        def mm(j):
+        def mm(j, *halves):
             g, jj = j // GT, j % GT
-            pa = psp.tile([P, 512], F32, tag="pa", name="pa%d" % j)
-            pb = psp.tile([P, 512], F32, tag="pb", name="pb%d" % j)
-            for h, bank in ((0, pa), (1, pb)):
+            for h in halves or (0, 1):
+                bank = psp.tile([P, 512], F32, tag=("pa", "pb")[h], name="p%d_%d" % (h, j))
+                prod[(j, h)] = bank
                 nc.tensor.matmul_mx(out=bank[:],
                                     lhsT=codes[g][:, jj * P:(jj + 1) * P].bitcast(FP8X4),
                                     lhsT_scale=scl[g][:, jj * P:(jj + 1) * P],
                                     rhs=w_codes[:, h * 512:(h + 1) * 512].bitcast(FP8X4),
                                     rhs_scale=w_scl[:, h * 512:(h + 1) * 512],
                                     start=True, stop=True)
-            prod[j] = (pa, pb)
 
         def gcol(j, t):
             return gs[:, j * E + t:j * E + t + 1]
@@ -147,7 +146,7 @@ def tile_sinelayer_loe_pa_t_kernel(tc, in_feats, tile_gate, W, out):
         b_t = {}
 
         def s_products(j):
-            pa = prod[j][0]
+            pa = prod[(j, 0)]
             for t in range(2):
                 s = spool.tile([P, COUT], F32, tag="s%d" % t, name="s%d_%d" % (t, j))
                 nc.scalar.activation(out=s[:], in_=pa[:, t * COUT:(t + 1) * COUT], func=ACT.Copy,
@@ -155,7 +154,7 @@ def tile_sinelayer_loe_pa_t_kernel(tc, in_feats, tile_gate, W, out):
                 s_t[(j, t)] = s
 
         def v_products(j):
-            pb = prod[j][1]
+            pb = prod[(j, 1)]
             for t in range(2):
                 b = spool.tile([P, COUT], F32, tag="b%d" % t, name="b%d_%d" % (t, j))
                 nc.vector.scalar_tensor_tensor(out=b[:], in0=pb[:, t * COUT:(t + 1) * COUT],
@@ -193,9 +192,9 @@ def tile_sinelayer_loe_pa_t_kernel(tc, in_feats, tile_gate, W, out):
         regroup("s", w_grp_f32, 0, wt0)
         wt1 = w_transpose(1)
         regroup("v", w_grp_f32, 1, wt1)
-        quant(w_codes, w_scl, w_grp, 0, 4)
         x_transpose(0, 0)
         x_exit("s", 0, 0)
+        quant(w_codes, w_scl, w_grp, 0, 4)
         x_quant(0, 0, 2)
         wt2 = w_transpose(2)
         regroup("s", w_grp_f32, 2, wt2)
@@ -205,12 +204,31 @@ def tile_sinelayer_loe_pa_t_kernel(tc, in_feats, tile_gate, W, out):
         x_transpose(0, 1)
         x_exit("s", 0, 1)
         x_quant(0, 2, 4)
-        for h in range(2):
-            x_transpose(1, h)
-            x_exit("s", 1, h)
+
+        mm(0, 0)
+        mm(1, 0)
+        x_transpose(1, 0)
+        mm(0, 1)
+        x_transpose(1, 1)
+        mm(1, 1)
+        for j in range(GT):
+            if j == 2:
+                mm(2)
+                x_transpose(2, 0)
+                mm(3)
+                x_transpose(2, 1)
+            s_products(j)
+            if j % 2 == 0:
+                x_exit("s", 1 + j // 2, 0)
+            v_products(j)
+            add("g", j)
+            if j % 2 == 1:
+                x_exit("v", 1 + j // 2, 1)
+            if j == 2:
+                x_quant(1, 0, GT)
 
         H = GW // 2
-        for g in range(NG):
+        for g in range(1, NG):
             last = g == NG - 1
             for s in range(GT):
                 j = g * GT + s
@@ -232,34 +250,36 @@ def tile_sinelayer_loe_pa_t_kernel(tc, in_feats, tile_gate, W, out):
                         sine(g - 2, s * H, (s + 1) * H)
                         if s == 1:
                             store(g - 2, 0, GW)
-                    if s == 3:
-                        sine(g - 1, 0, H)
                 v_products(j)
                 if not (last and s == 3):
                     add("g", j)
                 if not last:
                     if s == 0:
                         x_quant(g + 1, 0, GT)
-                    elif g >= 1:
-                        if s == 1:
-                            cast(g - 1, 0, GW)
-                        else:
-                            sub(g - 1, (s - 2) * H, (s - 1) * H)
-                else:
-                    if s == 0:
+                    elif s == 1:
                         cast(g - 1, 0, GW)
-                    elif s < 3:
-                        sub(g - 1, (s - 1) * H, s * H)
                     else:
-                        cast(g, 0, 2 * COUT)
-                        add("v", j)
-                        sub(g, 0, 2 * COUT)
-                        cast(g, 2 * COUT, 4 * COUT)
-                        sine(g - 1, H, GW)
-                        store(g - 1, 0, GW)
-                        sine(g, 0, 2 * COUT)
-                        store(g, 0, 2 * COUT)
-                        for q in range(2, GT):
-                            sub(g, q * COUT, (q + 1) * COUT)
-                            sine(g, q * COUT, (q + 1) * COUT)
-                            store(g, q * COUT, (q + 1) * COUT)
+                        sub(g - 1, (s - 2) * H, (s - 1) * H)
+                elif s == 0:
+                    cast(g - 1, 0, GW)
+                elif s == 1:
+                    sub(g - 1, 0, H)
+                    sub(g - 1, H, GW)
+                elif s == 2:
+                    cast(g, 0, COUT)
+                    sine(g - 1, 0, H)
+                    sub(g, 0, COUT)
+                else:
+                    sine(g - 1, H, GW)
+                    store(g - 1, 0, GW)
+                    sine(g, 0, COUT)
+                    store(g, 0, COUT)
+                    cast(g, COUT, 3 * COUT)
+                    add("v", j)
+                    sub(g, COUT, 3 * COUT)
+                    cast(g, 3 * COUT, GW)
+                    sine(g, COUT, 3 * COUT)
+                    store(g, COUT, 3 * COUT)
+                    sub(g, 3 * COUT, GW)
+                    sine(g, 3 * COUT, GW)
+                    store(g, 3 * COUT, GW)

@@ -19,6 +19,7 @@ NT = B // P
 GT = 4
 NG = NT // GT
 GW = GT * COUT
+W2 = 144
 FLOPS = 2 * B * CIN * COUT * E
 
 
@@ -33,10 +34,12 @@ def tile_sinelayer_loe_pa_t_kernel(tc, in_feats, tile_gate, W, out):
         ctx.enter_context(tc.manual_schedule())
         const = ctx.enter_context(tc.tile_pool(name="const", bufs=1))
         gpool = ctx.enter_context(tc.tile_pool(name="gpool", bufs=4))
-        spool = ctx.enter_context(tc.tile_pool(name="spool", bufs=5))
+        spool = ctx.enter_context(tc.tile_pool(name="spool", bufs=4))
         rpool = ctx.enter_context(tc.tile_pool(name="rpool", bufs=3))
+        kpool = ctx.enter_context(tc.tile_pool(name="kpool", bufs=1))
         psx = ctx.enter_context(tc.psum_pool(name="psx", bufs=2))
-        psp = ctx.enter_context(tc.psum_pool(name="psp", bufs=3))
+        psa = ctx.enter_context(tc.psum_pool(name="psa", bufs=3))
+        psb = ctx.enter_context(tc.psum_pool(name="psb", bufs=3))
 
         w_sb = const.tile([P, 8 * CIN], BF16, name="w_sb")
         w_sb3 = w_sb[:].rearrange("p (a k) -> p a k", a=8)
@@ -107,7 +110,7 @@ def tile_sinelayer_loe_pa_t_kernel(tc, in_feats, tile_gate, W, out):
         prod = {}
 
         def w_transpose(q):
-            wt = psp.tile([P, 512], F32, tag=("pa" if q % 2 == 0 else "pb"), name="wt%d" % q)
+            wt = (psa, psb)[q % 2].tile([P, 512], F32, tag=("pa", "pb")[q % 2], name="wt%d" % q)
             transposes(wt, w_f32, 2 * q)
             return wt
 
@@ -130,7 +133,7 @@ def tile_sinelayer_loe_pa_t_kernel(tc, in_feats, tile_gate, W, out):
         def mm(j, *halves):
             g, jj = j // GT, j % GT
             for h in halves or (0, 1):
-                bank = psp.tile([P, 512], F32, tag=("pa", "pb")[h], name="p%d_%d" % (h, j))
+                bank = (psa, psb)[h].tile([P, 512], F32, tag=("pa", "pb")[h], name="p%d_%d" % (h, j))
                 prod[(j, h)] = bank
                 nc.tensor.matmul_mx(out=bank[:],
                                     lhsT=codes[g][:, jj * P:(jj + 1) * P].bitcast(FP8X4),
@@ -146,36 +149,65 @@ def tile_sinelayer_loe_pa_t_kernel(tc, in_feats, tile_gate, W, out):
         b_t = {}
 
         def s_products(j):
-            pa = prod[(j, 0)]
-            for t in range(2):
-                s = spool.tile([P, COUT], F32, tag="s%d" % t, name="s%d_%d" % (t, j))
-                nc.scalar.activation(out=s[:], in_=pa[:, t * COUT:(t + 1) * COUT], func=ACT.Copy,
-                                     scale=gcol(j, t))
-                s_t[(j, t)] = s
+            a = spool.tile([P, COUT], F32, tag="a", name="a%d" % j)
+            nc.scalar.activation(out=a[:], in_=prod[(j, 0)][:, 0:COUT], func=ACT.Copy, scale=gcol(j, 0))
+            w2 = split(j)
+            if w2 > 0:
+                s = spool.tile([P, W2], F32, tag="s", name="s%d" % j)
+                nc.scalar.activation(out=s[:], in_=prod[(j, 0)][:, COUT:COUT + w2], func=ACT.Copy,
+                                     scale=gcol(j, 1))
+                s_t[(j, "s")] = s
+            s_t[(j, "a")] = a
 
-        def v_products(j):
-            pb = prod[(j, 1)]
-            for t in range(2):
-                b = spool.tile([P, COUT], F32, tag="b%d" % t, name="b%d_%d" % (t, j))
-                nc.vector.scalar_tensor_tensor(out=b[:], in0=pb[:, t * COUT:(t + 1) * COUT],
-                                               scalar=gcol(j, 2 + t), in1=s_t[(j, t)][:],
-                                               op0=ALU.mult, op1=ALU.add)
-                b_t[(j, t)] = b
+        def split(j):
+            return W2 if j < NT - GT else 0
 
-        def add(eng, j):
-            g, jj = j // GT, j % GT
-            if jj == 0:
+        def stt(dst, j, t, lo, hi, add):
+            nc.vector.scalar_tensor_tensor(out=dst,
+                                           in0=prod[(j, t // 2)][:, (t % 2) * COUT + lo:(t % 2) * COUT + hi],
+                                           scalar=gcol(j, t), in1=add, op0=ALU.mult, op1=ALU.add)
+
+        def v_c(j):
+            w2 = split(j)
+            a = s_t[(j, "a")]
+            stt(a[:, w2:COUT], j, 1, w2, COUT, a[:, w2:COUT])
+
+        def group_tiles(g):
+            if g not in u_t:
                 u_t[g] = rpool.tile([P, GW], F32, tag="u", name="u%d" % g)
-            e = nc.gpsimd if eng == "g" else nc.vector
-            e.tensor_tensor(out=u_t[g][:, jj * COUT:(jj + 1) * COUT], in0=b_t[(j, 0)][:],
-                            in1=b_t[(j, 1)][:], op=ALU.add)
+                b_t[(g, 0)] = rpool.tile([P, GW], F32, tag="b0", name="b0_%d" % g)
+                b_t[(g, 1)] = rpool.tile([P, GT * W2], F32, tag="b1", name="b1_%d" % g)
 
-        def cast(g, lo, hi):
-            if lo == 0:
-                k_t[g] = rpool.tile([P, GW], I32, tag="k", name="k%d" % g)
+        def v_b1(j):
+            g, jj = j // GT, j % GT
+            group_tiles(g)
+            if split(j) > 0:
+                stt(b_t[(g, 1)][:, jj * W2:(jj + 1) * W2], j, 3, 0, W2, s_t[(j, "s")][:])
+
+        def v_b0(j):
+            g, jj = j // GT, j % GT
+            stt(b_t[(g, 0)][:, jj * COUT:(jj + 1) * COUT], j, 2, 0, COUT, s_t[(j, "a")][:])
+
+        def v_u(j):
+            g, jj = j // GT, j % GT
+            lo, hi = jj * COUT + split(j), (jj + 1) * COUT
+            stt(u_t[g][:, lo:hi], j, 3, split(j), COUT, b_t[(g, 0)][:, lo:hi])
+
+        def add(g):
+            nc.gpsimd.tensor_tensor(out=u_t[g][:].rearrange("p (a c) -> p a c", a=GT)[:, :, 0:W2],
+                                    in0=b_t[(g, 0)][:].rearrange("p (a c) -> p a c", a=GT)[:, :, 0:W2],
+                                    in1=b_t[(g, 1)][:].rearrange("p (a c) -> p a c", a=GT)[:, :, 0:W2], op=ALU.add)
+
+        def cast(eng, g, lo, hi):
+            if g not in k_t:
+                k_t[g] = kpool.tile([P, GW], I32, tag="k", name="k%d" % g)
                 r_t[g] = rpool.tile([P, GW], F32, tag="r", name="r%d" % g)
                 o_t[g] = rpool.tile([P, GW], F32, tag="o", name="o%d" % g)
-            nc.vector.tensor_copy(out=k_t[g][:, lo:hi], in_=u_t[g][:, lo:hi])
+            if eng == "g":
+                nc.gpsimd.tensor_scalar(out=k_t[g][:, lo:hi], in0=u_t[g][:, lo:hi], scalar1=1.0, scalar2=0.0,
+                                        op0=ALU.mult, op1=ALU.add)
+            else:
+                nc.vector.tensor_copy(out=k_t[g][:, lo:hi], in_=u_t[g][:, lo:hi])
 
         def sub(g, lo, hi):
             nc.vector.tensor_tensor(out=r_t[g][:, lo:hi], in0=u_t[g][:, lo:hi],
@@ -205,81 +237,75 @@ def tile_sinelayer_loe_pa_t_kernel(tc, in_feats, tile_gate, W, out):
         x_exit("s", 0, 1)
         x_quant(0, 2, 4)
 
-        mm(0, 0)
-        mm(1, 0)
-        x_transpose(1, 0)
-        mm(0, 1)
-        x_transpose(1, 1)
-        mm(1, 1)
-        for j in range(GT):
-            if j == 2:
-                mm(2)
-                x_transpose(2, 0)
-                mm(3)
-                x_transpose(2, 1)
-            s_products(j)
-            if j % 2 == 0:
-                x_exit("s", 1 + j // 2, 0)
-            v_products(j)
-            add("g", j)
-            if j % 2 == 1:
-                x_exit("v", 1 + j // 2, 1)
-            if j == 2:
-                x_quant(1, 0, GT)
 
         H = GW // 2
-        for g in range(1, NG):
+        C = COUT
+        for g in range(NG):
             last = g == NG - 1
             for s in range(GT):
                 j = g * GT + s
-                if s % 2 == 0:
+                if g == 0:
+                    if s == 0:
+                        mm(0, 0)
+                        mm(1, 0)
+                        x_transpose(1, 0)
+                        mm(0, 1)
+                        x_transpose(1, 1)
+                        mm(1, 1)
+                    elif s == 2:
+                        mm(2)
+                        x_transpose(2, 0)
+                        mm(3)
+                        x_transpose(2, 1)
+                elif s % 2 == 0:
                     if g + 2 < NG:
                         x_transpose(g + 2, s // 2)
                     mm(j)
                     mm(j + 1)
                 s_products(j)
-                if not last:
-                    if s % 2 == 1 and g + 2 < NG:
-                        x_exit("s", g + 2, s // 2)
-                    if s % 2 == 0 and g >= 2:
-                        sine(g - 2, (s // 2) * H, (s // 2 + 1) * H)
-                        if s == 2:
-                            store(g - 2, 0, GW)
-                else:
-                    if s < 2:
-                        sine(g - 2, s * H, (s + 1) * H)
-                        if s == 1:
-                            store(g - 2, 0, GW)
-                v_products(j)
-                if not (last and s == 3):
-                    add("g", j)
-                if not last:
-                    if s == 0:
-                        x_quant(g + 1, 0, GT)
-                    elif s == 1:
-                        cast(g - 1, 0, GW)
-                    else:
-                        sub(g - 1, (s - 2) * H, (s - 1) * H)
-                elif s == 0:
-                    cast(g - 1, 0, GW)
-                elif s == 1:
-                    sub(g - 1, 0, H)
-                    sub(g - 1, H, GW)
-                elif s == 2:
-                    cast(g, 0, COUT)
-                    sine(g - 1, 0, H)
-                    sub(g, 0, COUT)
-                else:
-                    sine(g - 1, H, GW)
-                    store(g - 1, 0, GW)
-                    sine(g, 0, COUT)
-                    store(g, 0, COUT)
-                    cast(g, COUT, 3 * COUT)
-                    add("v", j)
-                    sub(g, COUT, 3 * COUT)
-                    cast(g, 3 * COUT, GW)
-                    sine(g, COUT, 3 * COUT)
-                    store(g, COUT, 3 * COUT)
-                    sub(g, 3 * COUT, GW)
-                    sine(g, 3 * COUT, GW)
-                    store(g, 3 * COUT, GW)
+                if g == 0:
+                    x_exit("s", 1 + s // 2, s % 2)
+                elif s % 2 == 0 and g + 2 < NG:
+                    x_exit("s", g + 2, s // 2)
+                if s % 2 == 1 and g >= 3:
+                    sine(g - 3, (s // 2) * H, (s // 2 + 1) * H)
+                    if s == 3:
+                        store(g - 3, 0, GW)
+                v_c(j)
+                if j > 0:
+                    v_u(j - 1)
+                v_b1(j)
+                v_b0(j)
+                if g == 0 and s == 1:
+                    x_quant(1, 0, GT)
+                if s == 1 and g >= 2:
+                    sub(g - 2, 0, GW)
+                if s == 3 and g + 2 < NG:
+                    x_quant(g + 2, 0, GT)
+                if s == 3 and not last:
+                    add(g)
+                if s == 1 and 1 <= g < NG - 1:
+                    cast("g", g - 1, 0, GW)
+                if last and s == 2:
+                    sine(g - 2, 0, H)
+                    cast("v", g - 1, 0, GW)
+        g = NG - 1
+        sine(g - 2, H, GW)
+        store(g - 2, 0, GW)
+        sub(g - 1, 0, H)
+        v_u(NT - 1)
+        sine(g - 1, 0, H)
+        sub(g - 1, H, GW)
+        sine(g - 1, H, GW)
+        store(g - 1, 0, GW)
+        cast("v", g, 0, 3 * C)
+        cast("v", g, 3 * C, GW)
+        sub(g, 0, 2 * C)
+        sine(g, 0, 2 * C)
+        store(g, 0, 2 * C)
+        sub(g, 2 * C, 3 * C)
+        sub(g, 3 * C, GW)
+        sine(g, 2 * C, 3 * C)
+        store(g, 2 * C, 3 * C)
+        sine(g, 3 * C, GW)
+        store(g, 3 * C, GW)

@@ -19,7 +19,7 @@ NT = B // P
 GT = 4
 NG = NT // GT
 GW = GT * COUT
-W2 = 144
+W2 = 160
 FLOPS = 2 * B * CIN * COUT * E
 
 
@@ -38,8 +38,8 @@ def tile_sinelayer_loe_pa_t_kernel(tc, in_feats, tile_gate, W, out):
         rpool = ctx.enter_context(tc.tile_pool(name="rpool", bufs=3))
         kpool = ctx.enter_context(tc.tile_pool(name="kpool", bufs=1))
         psx = ctx.enter_context(tc.psum_pool(name="psx", bufs=2))
-        psa = ctx.enter_context(tc.psum_pool(name="psa", bufs=3))
-        psb = ctx.enter_context(tc.psum_pool(name="psb", bufs=3))
+        psa = ctx.enter_context(tc.psum_pool(name="psa", bufs=2))
+        psb = ctx.enter_context(tc.psum_pool(name="psb", bufs=4))
 
         w_sb = const.tile([P, 8 * CIN], BF16, name="w_sb")
         w_sb3 = w_sb[:].rearrange("p (a k) -> p a k", a=8)
@@ -186,6 +186,7 @@ def tile_sinelayer_loe_pa_t_kernel(tc, in_feats, tile_gate, W, out):
 
         def v_b0(j):
             g, jj = j // GT, j % GT
+            group_tiles(g)
             stt(b_t[(g, 0)][:, jj * COUT:(jj + 1) * COUT], j, 2, 0, COUT, s_t[(j, "a")][:])
 
         def v_u(j):
@@ -240,55 +241,68 @@ def tile_sinelayer_loe_pa_t_kernel(tc, in_feats, tile_gate, W, out):
 
         H = GW // 2
         C = COUT
-        for g in range(NG):
+
+        def pe_pair(p):
+            g, h, j = p // 2, p % 2, 2 * p
+            if p == 0:
+                mm(0, 0)
+                mm(1, 0)
+                x_transpose(1, 0)
+                mm(0, 1)
+                x_transpose(1, 1)
+                mm(1, 1)
+            elif p == 1:
+                mm(2)
+                x_transpose(2, 0)
+                mm(3)
+                x_transpose(2, 1)
+            else:
+                if g + 2 < NG:
+                    x_transpose(g + 2, h)
+                mm(j)
+                mm(j + 1)
+
+        def s_step(j):
+            g, s = j // GT, j % GT
+            s_products(j)
+            if g == 0:
+                x_exit("s", 1 + s // 2, s % 2)
+            elif s % 2 == 0 and g + 2 < NG:
+                x_exit("s", g + 2, s // 2)
+            if s % 2 == 1 and g >= 3:
+                sine(g - 3, (s // 2) * H, (s // 2 + 1) * H)
+                if s == 3:
+                    store(g - 3, 0, GW)
+
+        pe_pair(0)
+        s_step(0)
+        v_c(0)
+        for j in range(NT):
+            g, s = j // GT, j % GT
             last = g == NG - 1
-            for s in range(GT):
-                j = g * GT + s
-                if g == 0:
-                    if s == 0:
-                        mm(0, 0)
-                        mm(1, 0)
-                        x_transpose(1, 0)
-                        mm(0, 1)
-                        x_transpose(1, 1)
-                        mm(1, 1)
-                    elif s == 2:
-                        mm(2)
-                        x_transpose(2, 0)
-                        mm(3)
-                        x_transpose(2, 1)
-                elif s % 2 == 0:
-                    if g + 2 < NG:
-                        x_transpose(g + 2, s // 2)
-                    mm(j)
-                    mm(j + 1)
-                s_products(j)
-                if g == 0:
-                    x_exit("s", 1 + s // 2, s % 2)
-                elif s % 2 == 0 and g + 2 < NG:
-                    x_exit("s", g + 2, s // 2)
-                if s % 2 == 1 and g >= 3:
-                    sine(g - 3, (s // 2) * H, (s // 2 + 1) * H)
-                    if s == 3:
-                        store(g - 3, 0, GW)
-                v_c(j)
-                if j > 0:
-                    v_u(j - 1)
-                v_b1(j)
-                v_b0(j)
-                if g == 0 and s == 1:
-                    x_quant(1, 0, GT)
-                if s == 1 and g >= 2:
-                    sub(g - 2, 0, GW)
-                if s == 3 and g + 2 < NG:
-                    x_quant(g + 2, 0, GT)
-                if s == 3 and not last:
-                    add(g)
-                if s == 1 and 1 <= g < NG - 1:
-                    cast("g", g - 1, 0, GW)
-                if last and s == 2:
-                    sine(g - 2, 0, H)
-                    cast("v", g - 1, 0, GW)
+            if j % 2 == 1 and j + 1 < NT:
+                pe_pair((j + 1) // 2)
+            if j + 1 < NT:
+                s_step(j + 1)
+            if j > 0:
+                v_u(j - 1)
+            v_b0(j)
+            if j + 1 < NT:
+                v_c(j + 1)
+            v_b1(j)
+            if g == 0 and s == 1:
+                x_quant(1, 0, GT)
+            if s == 1 and g >= 2:
+                sub(g - 2, 0, GW)
+            if s == 3 and g + 2 < NG:
+                x_quant(g + 2, 0, GT)
+            if s == 3 and not last:
+                add(g)
+            if s == 1 and 1 <= g < NG - 1:
+                cast("g", g - 1, 0, GW)
+            if last and s == 2:
+                sine(g - 2, 0, H)
+                cast("v", g - 1, 0, GW)
         g = NG - 1
         sine(g - 2, H, GW)
         store(g - 2, 0, GW)

@@ -19,7 +19,7 @@ NT = B // P
 GT = 4
 NG = NT // GT
 GW = GT * COUT
-W2 = 160
+W2 = 256
 FLOPS = 2 * B * CIN * COUT * E
 
 
@@ -34,12 +34,12 @@ def tile_sinelayer_loe_pa_t_kernel(tc, in_feats, tile_gate, W, out):
         ctx.enter_context(tc.manual_schedule())
         const = ctx.enter_context(tc.tile_pool(name="const", bufs=1))
         gpool = ctx.enter_context(tc.tile_pool(name="gpool", bufs=4))
-        spool = ctx.enter_context(tc.tile_pool(name="spool", bufs=4))
+        spool = ctx.enter_context(tc.tile_pool(name="spool", bufs=8))
         rpool = ctx.enter_context(tc.tile_pool(name="rpool", bufs=3))
-        kpool = ctx.enter_context(tc.tile_pool(name="kpool", bufs=1))
+        upool = ctx.enter_context(tc.tile_pool(name="upool", bufs=1))
         psx = ctx.enter_context(tc.psum_pool(name="psx", bufs=2))
-        psa = ctx.enter_context(tc.psum_pool(name="psa", bufs=2))
-        psb = ctx.enter_context(tc.psum_pool(name="psb", bufs=4))
+        psa = ctx.enter_context(tc.psum_pool(name="psa", bufs=3))
+        psb = ctx.enter_context(tc.psum_pool(name="psb", bufs=3))
 
         w_sb = const.tile([P, 8 * CIN], BF16, name="w_sb")
         w_sb3 = w_sb[:].rearrange("p (a k) -> p a k", a=8)
@@ -170,11 +170,14 @@ def tile_sinelayer_loe_pa_t_kernel(tc, in_feats, tile_gate, W, out):
         def v_c(j):
             w2 = split(j)
             a = s_t[(j, "a")]
+            if w2 == COUT:
+                return
             stt(a[:, w2:COUT], j, 1, w2, COUT, a[:, w2:COUT])
 
         def group_tiles(g):
-            if g not in u_t:
-                u_t[g] = rpool.tile([P, GW], F32, tag="u", name="u%d" % g)
+            if (g, 0) not in b_t:
+                if g == NG - 1:
+                    u_t[g] = const.tile([P, GW], F32, name="u_last")
                 b_t[(g, 0)] = rpool.tile([P, GW], F32, tag="b0", name="b0_%d" % g)
                 b_t[(g, 1)] = rpool.tile([P, GT * W2], F32, tag="b1", name="b1_%d" % g)
 
@@ -191,17 +194,20 @@ def tile_sinelayer_loe_pa_t_kernel(tc, in_feats, tile_gate, W, out):
 
         def v_u(j):
             g, jj = j // GT, j % GT
+            if split(j) == COUT:
+                return
             lo, hi = jj * COUT + split(j), (jj + 1) * COUT
             stt(u_t[g][:, lo:hi], j, 3, split(j), COUT, b_t[(g, 0)][:, lo:hi])
 
         def add(g):
+            u_t[g] = upool.tile([P, GW], F32, tag="u", name="u%d" % g)
             nc.gpsimd.tensor_tensor(out=u_t[g][:].rearrange("p (a c) -> p a c", a=GT)[:, :, 0:W2],
                                     in0=b_t[(g, 0)][:].rearrange("p (a c) -> p a c", a=GT)[:, :, 0:W2],
                                     in1=b_t[(g, 1)][:].rearrange("p (a c) -> p a c", a=GT)[:, :, 0:W2], op=ALU.add)
 
         def cast(eng, g, lo, hi):
             if g not in k_t:
-                k_t[g] = kpool.tile([P, GW], I32, tag="k", name="k%d" % g)
+                k_t[g] = rpool.tile([P, GW], I32, tag="k", name="k%d" % g)
                 r_t[g] = rpool.tile([P, GW], F32, tag="r", name="r%d" % g)
                 o_t[g] = rpool.tile([P, GW], F32, tag="o", name="o%d" % g)
             if eng == "g":
@@ -269,10 +275,10 @@ def tile_sinelayer_loe_pa_t_kernel(tc, in_feats, tile_gate, W, out):
                 x_exit("s", 1 + s // 2, s % 2)
             elif s % 2 == 0 and g + 2 < NG:
                 x_exit("s", g + 2, s // 2)
-            if s % 2 == 1 and g >= 3:
-                sine(g - 3, (s // 2) * H, (s // 2 + 1) * H)
+            if s % 2 == 1 and g >= 2:
+                sine(g - 2, (s // 2) * H, (s // 2 + 1) * H)
                 if s == 3:
-                    store(g - 3, 0, GW)
+                    store(g - 2, 0, GW)
 
         pe_pair(0)
         s_step(0)
@@ -292,20 +298,20 @@ def tile_sinelayer_loe_pa_t_kernel(tc, in_feats, tile_gate, W, out):
             v_b1(j)
             if g == 0 and s == 1:
                 x_quant(1, 0, GT)
-            if s == 1 and g >= 2:
-                sub(g - 2, 0, GW)
-            if s == 3 and g + 2 < NG:
-                x_quant(g + 2, 0, GT)
             if s == 3 and not last:
+                if g + 2 < NG:
+                    x_quant(g + 2, 0, 2)
+                if g >= 1:
+                    cast("v", g - 1, 0, H)
+                    cast("v", g - 1, H, GW)
+                    sub(g - 1, 0, H)
+                    sub(g - 1, H, GW)
+                if g + 2 < NG:
+                    x_quant(g + 2, 2, GT)
                 add(g)
-            if s == 1 and 1 <= g < NG - 1:
-                cast("g", g - 1, 0, GW)
             if last and s == 2:
-                sine(g - 2, 0, H)
                 cast("v", g - 1, 0, GW)
         g = NG - 1
-        sine(g - 2, H, GW)
-        store(g - 2, 0, GW)
         sub(g - 1, 0, H)
         v_u(NT - 1)
         sine(g - 1, 0, H)

@@ -38,8 +38,8 @@ def tile_sinelayer_loe_pa_t_kernel(tc, in_feats, tile_gate, W, out):
         rpool = ctx.enter_context(tc.tile_pool(name="rpool", bufs=3))
         upool = ctx.enter_context(tc.tile_pool(name="upool", bufs=1))
         psx = ctx.enter_context(tc.psum_pool(name="psx", bufs=2))
-        psa = ctx.enter_context(tc.psum_pool(name="psa", bufs=3))
-        psb = ctx.enter_context(tc.psum_pool(name="psb", bufs=3))
+        psa = ctx.enter_context(tc.psum_pool(name="psa", bufs=2))
+        psb = ctx.enter_context(tc.psum_pool(name="psb", bufs=4))
 
         w_sb = const.tile([P, 8 * CIN], BF16, name="w_sb")
         w_sb3 = w_sb[:].rearrange("p (a k) -> p a k", a=8)
@@ -65,6 +65,8 @@ def tile_sinelayer_loe_pa_t_kernel(tc, in_feats, tile_gate, W, out):
 
         ident = const.tile([P, P], F32, name="ident")
         make_identity(nc, ident[:])
+        zeros = const.tile([P, 512], BF16, name="zeros")
+        nc.vector.memset(zeros[:], 0.0)
         zero = const.tile([P, 1], F32, name="zero")
         nc.vector.memset(zero[:], 0.0)
         warm = const.tile([P, 1], F32, name="warm")
@@ -132,7 +134,7 @@ def tile_sinelayer_loe_pa_t_kernel(tc, in_feats, tile_gate, W, out):
 
         def mm(j, *halves):
             g, jj = j // GT, j % GT
-            for h in halves or (0, 1):
+            for h in halves or (1, 0):
                 bank = (psa, psb)[h].tile([P, 512], F32, tag=("pa", "pb")[h], name="p%d_%d" % (h, j))
                 prod[(j, h)] = bank
                 nc.tensor.matmul_mx(out=bank[:],
@@ -227,6 +229,13 @@ def tile_sinelayer_loe_pa_t_kernel(tc, in_feats, tile_gate, W, out):
         def store(g, lo, hi):
             nc.sync.dma_start(out=o_v[:, g * GW + lo:g * GW + hi], in_=o_t[g][:, lo:hi])
 
+        idle = psx.tile([P, 512], F32, tag="xt", name="idle")
+
+        def keep_warm(n):
+            for i in range(n):
+                nc.tensor.matmul(idle[:], lhsT=zeros[:, 0:P], rhs=zeros[:], start=(i == 0), stop=(i == n - 1))
+
+        keep_warm(3)
         wt0 = w_transpose(0)
         regroup("s", w_grp_f32, 0, wt0)
         wt1 = w_transpose(1)

@@ -19,7 +19,8 @@ NT = B // P
 GT = 4
 NG = NT // GT
 GW = GT * COUT
-W2 = 256
+C = COUT
+SP = 2
 FLOPS = 2 * B * CIN * COUT * E
 
 
@@ -36,7 +37,7 @@ def tile_sinelayer_loe_pa_t_kernel(tc, in_feats, tile_gate, W, out):
         gpool = ctx.enter_context(tc.tile_pool(name="gpool", bufs=4))
         spool = ctx.enter_context(tc.tile_pool(name="spool", bufs=8))
         rpool = ctx.enter_context(tc.tile_pool(name="rpool", bufs=3))
-        upool = ctx.enter_context(tc.tile_pool(name="upool", bufs=1))
+        kpool = ctx.enter_context(tc.tile_pool(name="kpool", bufs=1))
         psx = ctx.enter_context(tc.psum_pool(name="psx", bufs=2))
         psa = ctx.enter_context(tc.psum_pool(name="psa", bufs=2))
         psb = ctx.enter_context(tc.psum_pool(name="psb", bufs=4))
@@ -147,86 +148,71 @@ def tile_sinelayer_loe_pa_t_kernel(tc, in_feats, tile_gate, W, out):
         def gcol(j, t):
             return gs[:, j * E + t:j * E + t + 1]
 
+        a_t = {}
         s_t = {}
-        b_t = {}
+        b1_t = {}
+
+        def is_split(j):
+            return j % GT < SP and j < NT - GT
 
         def s_products(j):
-            a = spool.tile([P, COUT], F32, tag="a", name="a%d" % j)
-            nc.scalar.activation(out=a[:], in_=prod[(j, 0)][:, 0:COUT], func=ACT.Copy, scale=gcol(j, 0))
-            w2 = split(j)
-            if w2 > 0:
-                s = spool.tile([P, W2], F32, tag="s", name="s%d" % j)
-                nc.scalar.activation(out=s[:], in_=prod[(j, 0)][:, COUT:COUT + w2], func=ACT.Copy,
+            a_t[j] = spool.tile([P, C], F32, tag="a", name="a%d" % j)
+            nc.scalar.activation(out=a_t[j][:], in_=prod[(j, 0)][:, 0:C], func=ACT.Copy, scale=gcol(j, 0))
+            if is_split(j):
+                s_t[j] = spool.tile([P, C], F32, tag="s", name="s%d" % j)
+                nc.scalar.activation(out=s_t[j][:], in_=prod[(j, 0)][:, C:2 * C], func=ACT.Copy,
                                      scale=gcol(j, 1))
-                s_t[(j, "s")] = s
-            s_t[(j, "a")] = a
 
-        def split(j):
-            return W2 if j < NT - GT else 0
-
-        def stt(dst, j, t, lo, hi, add):
-            nc.vector.scalar_tensor_tensor(out=dst,
-                                           in0=prod[(j, t // 2)][:, (t % 2) * COUT + lo:(t % 2) * COUT + hi],
+        def stt(dst, j, t, add):
+            nc.vector.scalar_tensor_tensor(out=dst, in0=prod[(j, t // 2)][:, (t % 2) * C:(t % 2 + 1) * C],
                                            scalar=gcol(j, t), in1=add, op0=ALU.mult, op1=ALU.add)
 
-        def v_c(j):
-            w2 = split(j)
-            a = s_t[(j, "a")]
-            if w2 == COUT:
-                return
-            stt(a[:, w2:COUT], j, 1, w2, COUT, a[:, w2:COUT])
+        def ucol(j):
+            g, jj = j // GT, j % GT
+            return u_t[g][:, jj * C:(jj + 1) * C]
 
-        def group_tiles(g):
-            if (g, 0) not in b_t:
-                if g == NG - 1:
-                    u_t[g] = const.tile([P, GW], F32, name="u_last")
-                b_t[(g, 0)] = rpool.tile([P, GW], F32, tag="b0", name="b0_%d" % g)
-                b_t[(g, 1)] = rpool.tile([P, GT * W2], F32, tag="b1", name="b1_%d" % g)
+        def v_c(j):
+            stt(a_t[j][:], j, 1, a_t[j][:])
+
+        def v_b0(j):
+            g = j // GT
+            if g not in u_t:
+                u_t[g] = rpool.tile([P, GW], F32, tag="u", name="u%d" % g)
+            stt(ucol(j), j, 2, a_t[j][:])
 
         def v_b1(j):
             g, jj = j // GT, j % GT
-            group_tiles(g)
-            if split(j) > 0:
-                stt(b_t[(g, 1)][:, jj * W2:(jj + 1) * W2], j, 3, 0, W2, s_t[(j, "s")][:])
-
-        def v_b0(j):
-            g, jj = j // GT, j % GT
-            group_tiles(g)
-            stt(b_t[(g, 0)][:, jj * COUT:(jj + 1) * COUT], j, 2, 0, COUT, s_t[(j, "a")][:])
+            if jj == 0:
+                b1_t[g] = rpool.tile([P, SP * C], F32, tag="b1", name="b1_%d" % g)
+            stt(b1_t[g][:, jj * C:(jj + 1) * C], j, 3, s_t[j][:])
 
         def v_u(j):
-            g, jj = j // GT, j % GT
-            if split(j) == COUT:
-                return
-            lo, hi = jj * COUT + split(j), (jj + 1) * COUT
-            stt(u_t[g][:, lo:hi], j, 3, split(j), COUT, b_t[(g, 0)][:, lo:hi])
+            stt(ucol(j), j, 3, ucol(j))
 
         def add(g):
-            u_t[g] = upool.tile([P, GW], F32, tag="u", name="u%d" % g)
-            nc.gpsimd.tensor_tensor(out=u_t[g][:].rearrange("p (a c) -> p a c", a=GT)[:, :, 0:W2],
-                                    in0=b_t[(g, 0)][:].rearrange("p (a c) -> p a c", a=GT)[:, :, 0:W2],
-                                    in1=b_t[(g, 1)][:].rearrange("p (a c) -> p a c", a=GT)[:, :, 0:W2], op=ALU.add)
+            nc.gpsimd.tensor_tensor(out=u_t[g][:, 0:SP * C], in0=u_t[g][:, 0:SP * C], in1=b1_t[g][:], op=ALU.add)
 
-        def cast(eng, g, lo, hi):
+        def cast(g):
+            k_t[g] = kpool.tile([P, GW], I32, tag="k", name="k%d" % g)
+            nc.gpsimd.tensor_scalar(out=k_t[g][:], in0=u_t[g][:], scalar1=1.0, scalar2=0.0,
+                                    op0=ALU.mult, op1=ALU.add)
+
+        def v_cast(g, lo, hi):
             if g not in k_t:
-                k_t[g] = rpool.tile([P, GW], I32, tag="k", name="k%d" % g)
-                r_t[g] = rpool.tile([P, GW], F32, tag="r", name="r%d" % g)
-                o_t[g] = rpool.tile([P, GW], F32, tag="o", name="o%d" % g)
-            if eng == "g":
-                nc.gpsimd.tensor_scalar(out=k_t[g][:, lo:hi], in0=u_t[g][:, lo:hi], scalar1=1.0, scalar2=0.0,
-                                        op0=ALU.mult, op1=ALU.add)
-            else:
-                nc.vector.tensor_copy(out=k_t[g][:, lo:hi], in_=u_t[g][:, lo:hi])
+                k_t[g] = const.tile([P, GW], I32, name="k_last")
+            nc.vector.tensor_copy(out=k_t[g][:, lo:hi], in_=u_t[g][:, lo:hi])
 
         def sub(g, lo, hi):
+            if lo == 0:
+                r_t[g] = rpool.tile([P, GW], F32, tag="r", name="r%d" % g)
             nc.vector.tensor_tensor(out=r_t[g][:, lo:hi], in0=u_t[g][:, lo:hi],
                                     in1=k_t[g][:, lo:hi], op=ALU.subtract)
 
         def sine(g, lo, hi):
+            if lo == 0:
+                o_t[g] = rpool.tile([P, GW], F32, tag="o", name="o%d" % g)
             nc.scalar.activation(out=o_t[g][:, lo:hi], in_=r_t[g][:, lo:hi], func=ACT.Sin,
                                  scale=2.0 * math.pi)
-
-        def store(g, lo, hi):
             nc.sync.dma_start(out=o_v[:, g * GW + lo:g * GW + hi], in_=o_t[g][:, lo:hi])
 
         idle = psx.tile([P, 512], F32, tag="xt", name="idle")
@@ -254,19 +240,16 @@ def tile_sinelayer_loe_pa_t_kernel(tc, in_feats, tile_gate, W, out):
         x_quant(0, 2, 4)
 
 
-        H = GW // 2
-        C = COUT
-
-        def pe_pair(p):
-            g, h, j = p // 2, p % 2, 2 * p
-            if p == 0:
+        def passes(g, h):
+            j = GT * g + 2 * h
+            if g == 0 and h == 0:
                 mm(0, 0)
                 mm(1, 0)
                 x_transpose(1, 0)
                 mm(0, 1)
                 x_transpose(1, 1)
                 mm(1, 1)
-            elif p == 1:
+            elif g == 0:
                 mm(2)
                 x_transpose(2, 0)
                 mm(3)
@@ -277,64 +260,73 @@ def tile_sinelayer_loe_pa_t_kernel(tc, in_feats, tile_gate, W, out):
                 mm(j)
                 mm(j + 1)
 
-        def s_step(j):
-            g, s = j // GT, j % GT
-            s_products(j)
-            if g == 0:
-                x_exit("s", 1 + s // 2, s % 2)
-            elif s % 2 == 0 and g + 2 < NG:
-                x_exit("s", g + 2, s // 2)
-            if s % 2 == 1 and g >= 2:
-                sine(g - 2, (s // 2) * H, (s // 2 + 1) * H)
-                if s == 3:
-                    store(g - 2, 0, GW)
+        def scalar_half(g, h):
+            for jj in (2 * h, 2 * h + 1):
+                s_products(GT * g + jj)
+                if g == 0:
+                    x_exit("s", 1 + jj // 2, jj % 2)
+                elif jj % 2 == 0 and g + 2 < NG:
+                    x_exit("s", g + 2, h)
 
-        pe_pair(0)
-        s_step(0)
-        v_c(0)
-        for j in range(NT):
-            g, s = j // GT, j % GT
-            last = g == NG - 1
-            if j % 2 == 1 and j + 1 < NT:
-                pe_pair((j + 1) // 2)
-            if j + 1 < NT:
-                s_step(j + 1)
-            if j > 0:
-                v_u(j - 1)
-            v_b0(j)
-            if j + 1 < NT:
+        def front(g):
+            j = GT * g
+            passes(g, 0)
+            scalar_half(g, 0)
+            if g == NG - 1:
+                v_c(j)
                 v_c(j + 1)
+            passes(g, 1)
+            scalar_half(g, 1)
+            if g >= 2:
+                sine(g - 2, 0, GW)
+
+        front(0)
+        for g in range(NG - 1):
+            j = GT * g
+            if g >= 1:
+                cast(g - 1)
+            v_b0(j)
             v_b1(j)
-            if g == 0 and s == 1:
+            v_b0(j + 1)
+            v_b1(j + 1)
+            add(g)
+            v_c(j + 2)
+            v_c(j + 3)
+            v_b0(j + 2)
+            v_b0(j + 3)
+            if g == 0:
                 x_quant(1, 0, GT)
-            if s == 3 and not last:
-                if g + 2 < NG:
-                    x_quant(g + 2, 0, 2)
-                if g >= 1:
-                    cast("v", g - 1, 0, H)
-                    cast("v", g - 1, H, GW)
-                    sub(g - 1, 0, H)
-                    sub(g - 1, H, GW)
-                if g + 2 < NG:
-                    x_quant(g + 2, 2, GT)
-                add(g)
-            if last and s == 2:
-                cast("v", g - 1, 0, GW)
+            v_u(j + 2)
+            v_u(j + 3)
+            if g + 2 < NG:
+                x_quant(g + 2, 0, 2)
+            if g >= 1:
+                sub(g - 1, 0, GW)
+            if g + 2 < NG:
+                x_quant(g + 2, 2, GT)
+            front(g + 1)
+
         g = NG - 1
-        sub(g - 1, 0, H)
-        v_u(NT - 1)
-        sine(g - 1, 0, H)
-        sub(g - 1, H, GW)
-        sine(g - 1, H, GW)
-        store(g - 1, 0, GW)
-        cast("v", g, 0, 3 * C)
-        cast("v", g, 3 * C, GW)
+        j = GT * g
+        cast(g - 1)
+        v_b0(j)
+        v_b0(j + 1)
+        v_c(j + 2)
+        v_c(j + 3)
+        v_u(j)
+        v_u(j + 1)
+        v_b0(j + 2)
+        v_b0(j + 3)
+        v_cast(g, 0, 2 * C)
+        sub(g - 1, 0, GW)
+        sine(g - 1, 0, GW)
+        v_u(j + 2)
+        v_u(j + 3)
         sub(g, 0, 2 * C)
         sine(g, 0, 2 * C)
-        store(g, 0, 2 * C)
+        v_cast(g, 2 * C, 3 * C)
+        v_cast(g, 3 * C, GW)
         sub(g, 2 * C, 3 * C)
-        sub(g, 3 * C, GW)
         sine(g, 2 * C, 3 * C)
-        store(g, 2 * C, 3 * C)
+        sub(g, 3 * C, GW)
         sine(g, 3 * C, GW)
-        store(g, 3 * C, GW)

@@ -23,7 +23,6 @@ C = COUT
 SP = 2
 FLOPS = 2 * B * CIN * COUT * E
 
-
 def tile_sinelayer_loe_pa_t_kernel(tc, in_feats, tile_gate, W, out):
     nc = tc.nc
     x_v = in_feats.rearrange("(p r) k -> p (r k)", p=P)
@@ -153,7 +152,7 @@ def tile_sinelayer_loe_pa_t_kernel(tc, in_feats, tile_gate, W, out):
         b1_t = {}
 
         def is_split(j):
-            return j % GT < SP and j < NT - GT
+            return j % GT < SP and j >= GT
 
         def s_products(j):
             a_t[j] = spool.tile([P, C], F32, tag="a", name="a%d" % j)
@@ -203,13 +202,13 @@ def tile_sinelayer_loe_pa_t_kernel(tc, in_feats, tile_gate, W, out):
             nc.vector.tensor_copy(out=k_t[g][:, lo:hi], in_=u_t[g][:, lo:hi])
 
         def sub(g, lo, hi):
-            if lo == 0:
+            if g not in r_t:
                 r_t[g] = rpool.tile([P, GW], F32, tag="r", name="r%d" % g)
             nc.vector.tensor_tensor(out=r_t[g][:, lo:hi], in0=u_t[g][:, lo:hi],
                                     in1=k_t[g][:, lo:hi], op=ALU.subtract)
 
         def sine(g, lo, hi):
-            if lo == 0:
+            if g not in o_t:
                 o_t[g] = rpool.tile([P, GW], F32, tag="o", name="o%d" % g)
             nc.scalar.activation(out=o_t[g][:, lo:hi], in_=r_t[g][:, lo:hi], func=ACT.Sin,
                                  scale=2.0 * math.pi)
@@ -239,21 +238,26 @@ def tile_sinelayer_loe_pa_t_kernel(tc, in_feats, tile_gate, W, out):
         x_exit("s", 0, 1)
         x_quant(0, 2, 4)
 
-
         def passes(g, h):
             j = GT * g + 2 * h
             if g == 0 and h == 0:
                 mm(0, 0)
                 mm(1, 0)
                 x_transpose(1, 0)
-                mm(0, 1)
                 x_transpose(1, 1)
+                mm(0, 1)
                 mm(1, 1)
             elif g == 0:
-                mm(2)
+                mm(2, 0)
+                mm(3, 0)
                 x_transpose(2, 0)
-                mm(3)
+                mm(2, 1)
+                mm(3, 1)
                 x_transpose(2, 1)
+            elif g == 1:
+                mm(j)
+                mm(j + 1)
+                x_transpose(g + 2, h)
             else:
                 if g + 2 < NG:
                     x_transpose(g + 2, h)
@@ -261,18 +265,28 @@ def tile_sinelayer_loe_pa_t_kernel(tc, in_feats, tile_gate, W, out):
                 mm(j + 1)
 
         def scalar_half(g, h):
+            if g == 0:
+                if h == 0:
+                    s_products(0)
+                    s_products(1)
+                    x_exit("s", 1, 0)
+                    x_exit("s", 1, 1)
+                else:
+                    s_products(2)
+                    s_products(3)
+                    x_exit("s", 2, 0)
+                    x_exit("s", 2, 1)
+                return
             for jj in (2 * h, 2 * h + 1):
                 s_products(GT * g + jj)
-                if g == 0:
-                    x_exit("s", 1 + jj // 2, jj % 2)
-                elif jj % 2 == 0 and g + 2 < NG:
+                if jj % 2 == (g == 1) and g + 2 < NG:
                     x_exit("s", g + 2, h)
 
         def front(g):
             j = GT * g
             passes(g, 0)
             scalar_half(g, 0)
-            if g == NG - 1:
+            if g == 0:
                 v_c(j)
                 v_c(j + 1)
             passes(g, 1)
@@ -286,23 +300,29 @@ def tile_sinelayer_loe_pa_t_kernel(tc, in_feats, tile_gate, W, out):
             if g >= 1:
                 cast(g - 1)
             v_b0(j)
-            v_b1(j)
+            if g > 0:
+                v_b1(j)
             v_b0(j + 1)
-            v_b1(j + 1)
-            add(g)
+            if g > 0:
+                v_b1(j + 1)
+                add(g)
+            else:
+                v_u(j)
+                v_u(j + 1)
+                x_quant(1, 0, GT)
             v_c(j + 2)
             v_c(j + 3)
             v_b0(j + 2)
             v_b0(j + 3)
-            if g == 0:
-                x_quant(1, 0, GT)
             v_u(j + 2)
             v_u(j + 3)
-            if g + 2 < NG:
+            if g == 0:
+                x_quant(2, 0, GT)
+            elif g + 2 < NG:
                 x_quant(g + 2, 0, 2)
             if g >= 1:
                 sub(g - 1, 0, GW)
-            if g + 2 < NG:
+            if 0 < g < NG - 2:
                 x_quant(g + 2, 2, GT)
             front(g + 1)
 
@@ -310,23 +330,25 @@ def tile_sinelayer_loe_pa_t_kernel(tc, in_feats, tile_gate, W, out):
         j = GT * g
         cast(g - 1)
         v_b0(j)
+        v_b1(j)
         v_b0(j + 1)
+        v_b1(j + 1)
+        add(g)
         v_c(j + 2)
         v_c(j + 3)
-        v_u(j)
-        v_u(j + 1)
         v_b0(j + 2)
         v_b0(j + 3)
-        v_cast(g, 0, 2 * C)
-        sub(g - 1, 0, GW)
-        sine(g - 1, 0, GW)
         v_u(j + 2)
         v_u(j + 3)
-        sub(g, 0, 2 * C)
-        sine(g, 0, 2 * C)
-        v_cast(g, 2 * C, 3 * C)
-        v_cast(g, 3 * C, GW)
-        sub(g, 2 * C, 3 * C)
-        sine(g, 2 * C, 3 * C)
-        sub(g, 3 * C, GW)
-        sine(g, 3 * C, GW)
+        sub(g - 1, 0, 2 * C)
+        sine(g - 1, 0, 2 * C)
+        sub(g - 1, 2 * C, GW)
+        sine(g - 1, 2 * C, GW)
+        v_cast(g, 2 * C, GW)
+        v_cast(g, 0, 2 * C)
+        sub(g, 2 * C, GW)
+        sine(g, 2 * C, GW)
+        sub(g, 0, C)
+        sine(g, 0, C)
+        sub(g, C, 2 * C)
+        sine(g, C, 2 * C)

@@ -227,13 +227,15 @@ def tile_sinelayer_loe_pa_t_kernel(tc, in_feats, tile_gate, W, out):
         regroup("v", w_grp_f32, 1, wt1)
         x_transpose(0, 0)
         x_exit("s", 0, 0)
-        quant(w_codes, w_scl, w_grp, 0, 4)
+        quant(w_codes, w_scl, w_grp, 0, 2)
+        quant(w_codes, w_scl, w_grp, 2, 4)
         x_quant(0, 0, 2)
         wt2 = w_transpose(2)
         regroup("s", w_grp_f32, 2, wt2)
         wt3 = w_transpose(3)
         regroup("v", w_grp_f32, 3, wt3)
-        quant(w_codes, w_scl, w_grp, 4, 8)
+        quant(w_codes, w_scl, w_grp, 4, 6)
+        quant(w_codes, w_scl, w_grp, 6, 8)
         x_transpose(0, 1)
         x_exit("s", 0, 1)
         x_quant(0, 2, 4)
@@ -299,23 +301,30 @@ def tile_sinelayer_loe_pa_t_kernel(tc, in_feats, tile_gate, W, out):
             j = GT * g
             if g >= 1:
                 cast(g - 1)
-            v_b0(j)
-            if g > 0:
+            if g == 0:
+                v_b0(j)
+                v_b0(j + 1)
+                x_quant(1, 0, GT)
+                v_c(j + 2)
+                v_u(j)
+                v_c(j + 3)
+                v_u(j + 1)
+                v_b0(j + 2)
+                v_b0(j + 3)
+                v_u(j + 2)
+                v_u(j + 3)
+            else:
+                v_b0(j)
                 v_b1(j)
-            v_b0(j + 1)
-            if g > 0:
+                v_b0(j + 1)
                 v_b1(j + 1)
                 add(g)
-            else:
-                v_u(j)
-                v_u(j + 1)
-                x_quant(1, 0, GT)
-            v_c(j + 2)
-            v_c(j + 3)
-            v_b0(j + 2)
-            v_b0(j + 3)
-            v_u(j + 2)
-            v_u(j + 3)
+                v_c(j + 2)
+                v_c(j + 3)
+                v_b0(j + 2)
+                v_b0(j + 3)
+                v_u(j + 2)
+                v_u(j + 3)
             if g == 0:
                 x_quant(2, 0, GT)
             elif g + 2 < NG:
@@ -346,8 +355,10 @@ def tile_sinelayer_loe_pa_t_kernel(tc, in_feats, tile_gate, W, out):
         sine(g - 1, 2 * C, GW)
         v_cast(g, 2 * C, GW)
         v_cast(g, 0, 2 * C)
-        sub(g, 2 * C, GW)
-        sine(g, 2 * C, GW)
+        sub(g, 2 * C, 3 * C)
+        sine(g, 2 * C, 3 * C)
+        sub(g, 3 * C, GW)
+        sine(g, 3 * C, GW)
         sub(g, 0, C)
         sine(g, 0, C)
         sub(g, C, 2 * C)

import math
from contextlib import ExitStack

import concourse.mybir as mybir
from concourse.masks import make_identity

F32 = mybir.dt.float32
BF16 = mybir.dt.bfloat16
I32 = mybir.dt.int32
U32 = mybir.dt.uint32
U8 = mybir.dt.uint8
FP8X4 = mybir.dt.float8_e4m3fn_x4
ALU = mybir.AluOpType
ACT = mybir.ActivationFunctionType

P = 128
B, CIN, COUT, E = 8192, 512, 256, 4
NT = B // P
GT = 4
NG = NT // GT
GW = GT * COUT
C = COUT
SP = 2
FLOPS = 2 * B * CIN * COUT * E

def tile_sinelayer_loe_pa_t_kernel(tc, in_feats, tile_gate, W, out):
    nc = tc.nc
    x_v = in_feats.rearrange("(p r) k -> p (r k)", p=P)
    g_v = tile_gate.rearrange("(p r) e -> p (r e)", p=P)
    w_v = W.rearrange("t (h p) k -> p (t h) k", p=P)
    o_v = out.rearrange("(p r) c -> p (r c)", p=P)

    with ExitStack() as ctx:
        ctx.enter_context(tc.manual_schedule())
        const = ctx.enter_context(tc.tile_pool(name="const", bufs=1))
        gpool = ctx.enter_context(tc.tile_pool(name="gpool", bufs=4))
        spool = ctx.enter_context(tc.tile_pool(name="spool", bufs=8))
        rpool = ctx.enter_context(tc.tile_pool(name="rpool", bufs=3))
        kpool = ctx.enter_context(tc.tile_pool(name="kpool", bufs=1))
        psx = ctx.enter_context(tc.psum_pool(name="psx", bufs=2))
        psa = ctx.enter_context(tc.psum_pool(name="psa", bufs=2))
        psb = ctx.enter_context(tc.psum_pool(name="psb", bufs=4))

        w_sb = const.tile([P, 8 * CIN], BF16, name="w_sb")
        w_sb3 = w_sb[:].rearrange("p (a k) -> p a k", a=8)

        def load_w(q):
            nc.sync.dma_start(out=w_sb3[:, 2 * q:2 * q + 2, :], in_=w_v[:, 2 * q:2 * q + 2, :])

        gate_sb = const.tile([P, NT * E], BF16, name="gate_sb")
        nc.scalar.dma_start(out=gate_sb[:], in_=g_v)
        xs = []
        for g in range(NG):
            x_t = const.tile([P, GT * CIN], BF16, name="x%d" % g)
            xs.append(x_t)
        half = GT * CIN // 2
        load_w(0)
        load_w(1)
        nc.sync.dma_start(out=xs[0][:, 0:half], in_=x_v[:, 0:half])
        load_w(2)
        load_w(3)
        nc.sync.dma_start(out=xs[0][:, half:2 * half], in_=x_v[:, half:2 * half])
        for g in range(1, NG):
            nc.sync.dma_start(out=xs[g][:], in_=x_v[:, g * GT * CIN:(g + 1) * GT * CIN])

        ident = const.tile([P, P], F32, name="ident")
        make_identity(nc, ident[:])
        zeros = const.tile([P, 512], BF16, name="zeros")
        nc.vector.memset(zeros[:], 0.0)
        zero = const.tile([P, 1], F32, name="zero")
        nc.vector.memset(zero[:], 0.0)
        warm = const.tile([P, 1], F32, name="warm")
        nc.scalar.activation(out=warm[:], in_=zero[:], func=ACT.Sin)
        gs = const.tile([P, NT * E], F32, name="gs")
        nc.vector.tensor_scalar(out=gs[:], in0=gate_sb[:], scalar1=30.0 / (2.0 * math.pi),
                                scalar2=None, op0=ALU.mult)

        def transposes(bank, src_f32, first):
            for jj in range(2):
                for u in range(2):
                    c = (first + jj) * 256
                    nc.tensor.transpose(bank[:, (jj * 2 + u) * P:(jj * 2 + u + 1) * P],
                                        src_f32[:, c + u:c + 256:2], ident[:])

        def regroup(eng, grp_f32, h, bank):
            dst = grp_f32[:, h * 512:(h + 1) * 512].rearrange("p (j m u) -> p j m u", j=2, u=2)
            src = bank[:].rearrange("p (j u m) -> p j m u", j=2, u=2)
            if eng == "s":
                nc.scalar.copy(out=dst, in_=src)
            else:
                nc.vector.tensor_copy(out=dst, in_=src)

        def quant(codes, scl, grp, lo, hi):
            nc.vector.quantize_mx(out=codes[:, lo * P:hi * P].bitcast(FP8X4),
                                  scales=scl[:, lo * P:hi * P],
                                  in_=grp[:, lo * CIN:hi * CIN])

        w_f32 = w_sb[:].bitcast(F32)
        w_grp = const.tile([P, 8 * CIN], BF16, name="w_grp", align_bytes=64)
        w_grp_f32 = w_grp[:].bitcast(F32)
        w_codes = const.tile([P, E * COUT], U32, name="w_codes", align_bytes=64)
        w_scl = const.tile([P, E * COUT], U8, name="w_scl", align_bytes=64)

        grp = {}
        banks = {}
        codes = {}
        scl = {}
        u_t = {}
        o_t = {}
        k_t = {}
        r_t = {}
        prod = {}

        def w_transpose(q):
            wt = (psa, psb)[q % 2].tile([P, 512], F32, tag=("pa", "pb")[q % 2], name="wt%d" % q)
            transposes(wt, w_f32, 2 * q)
            return wt

        def x_transpose(g, h):
            if h == 0:
                grp[g] = gpool.tile([P, GT * CIN], BF16, tag="grp", name="grp%d" % g, align_bytes=64)
            bank = psx.tile([P, 512], F32, tag="xt", name="xt%d_%d" % (g, h))
            transposes(bank, xs[g][:].bitcast(F32), 2 * h)
            banks[(g, h)] = bank

        def x_exit(eng, g, h):
            regroup(eng, grp[g][:].bitcast(F32), h, banks[(g, h)])

        def x_quant(g, lo, hi):
            if lo == 0:
                codes[g] = gpool.tile([P, GT * P], U32, tag="codes", name="codes%d" % g, align_bytes=64)
                scl[g] = gpool.tile([P, GT * P], U8, tag="scl", name="scl%d" % g, align_bytes=64)
            quant(codes[g], scl[g], grp[g], lo, hi)

        def mm(j, *halves):
            g, jj = j // GT, j % GT
            for h in halves or (1, 0):
                bank = (psa, psb)[h].tile([P, 512], F32, tag=("pa", "pb")[h], name="p%d_%d" % (h, j))
                prod[(j, h)] = bank
                nc.tensor.matmul_mx(out=bank[:],
                                    lhsT=codes[g][:, jj * P:(jj + 1) * P].bitcast(FP8X4),
                                    lhsT_scale=scl[g][:, jj * P:(jj + 1) * P],
                                    rhs=w_codes[:, h * 512:(h + 1) * 512].bitcast(FP8X4),
                                    rhs_scale=w_scl[:, h * 512:(h + 1) * 512],
                                    start=True, stop=True)

        def gcol(j, t):
            return gs[:, j * E + t:j * E + t + 1]

        a_t = {}
        s_t = {}
        b1_t = {}

        def is_split(j):
            return j % GT < SP and j >= GT

        def s_products(j):
            a_t[j] = spool.tile([P, C], F32, tag="a", name="a%d" % j)
            nc.scalar.activation(out=a_t[j][:], in_=prod[(j, 0)][:, 0:C], func=ACT.Copy, scale=gcol(j, 0))
            if is_split(j):
                s_t[j] = spool.tile([P, C], F32, tag="s", name="s%d" % j)
                nc.scalar.activation(out=s_t[j][:], in_=prod[(j, 0)][:, C:2 * C], func=ACT.Copy,
                                     scale=gcol(j, 1))

        def stt(dst, j, t, add):
            nc.vector.scalar_tensor_tensor(out=dst, in0=prod[(j, t // 2)][:, (t % 2) * C:(t % 2 + 1) * C],
                                           scalar=gcol(j, t), in1=add, op0=ALU.mult, op1=ALU.add)

        def ucol(j):
            g, jj = j // GT, j % GT
            return u_t[g][:, jj * C:(jj + 1) * C]

        def v_c(j):
            stt(a_t[j][:], j, 1, a_t[j][:])

        def v_b0(j):
            g = j // GT
            if g not in u_t:
                u_t[g] = rpool.tile([P, GW], F32, tag="u", name="u%d" % g)
            stt(ucol(j), j, 2, a_t[j][:])

        def v_b1(j):
            g, jj = j // GT, j % GT
            if jj == 0:
                b1_t[g] = rpool.tile([P, SP * C], F32, tag="b1", name="b1_%d" % g)
            stt(b1_t[g][:, jj * C:(jj + 1) * C], j, 3, s_t[j][:])

        def v_u(j):
            stt(ucol(j), j, 3, ucol(j))

        def add(g):
            nc.gpsimd.tensor_tensor(out=u_t[g][:, 0:SP * C], in0=u_t[g][:, 0:SP * C], in1=b1_t[g][:], op=ALU.add)

        def cast(g):
            k_t[g] = kpool.tile([P, GW], I32, tag="k", name="k%d" % g)
            nc.gpsimd.tensor_scalar(out=k_t[g][:], in0=u_t[g][:], scalar1=1.0, scalar2=0.0,
                                    op0=ALU.mult, op1=ALU.add)

        def v_cast(g, lo, hi):
            if g not in k_t:
                k_t[g] = const.tile([P, GW], I32, name="k_last")
            nc.vector.tensor_copy(out=k_t[g][:, lo:hi], in_=u_t[g][:, lo:hi])

        def sub(g, lo, hi):
            if g not in r_t:
                r_t[g] = rpool.tile([P, GW], F32, tag="r", name="r%d" % g)
            nc.vector.tensor_tensor(out=r_t[g][:, lo:hi], in0=u_t[g][:, lo:hi],
                                    in1=k_t[g][:, lo:hi], op=ALU.subtract)

        def sine(g, lo, hi):
            if g not in o_t:
                o_t[g] = rpool.tile([P, GW], F32, tag="o", name="o%d" % g)
            nc.scalar.activation(out=o_t[g][:, lo:hi], in_=r_t[g][:, lo:hi], func=ACT.Sin,
                                 scale=2.0 * math.pi)
            nc.sync.dma_start(out=o_v[:, g * GW + lo:g * GW + hi], in_=o_t[g][:, lo:hi])

        idle = psx.tile([P, 512], F32, tag="xt", name="idle")

        def keep_warm(n):
            for i in range(n):
                nc.tensor.matmul(idle[:], lhsT=zeros[:, 0:P], rhs=zeros[:], start=(i == 0), stop=(i == n - 1))

        keep_warm(3)
        wt0 = w_transpose(0)
        regroup("s", w_grp_f32, 0, wt0)
        wt1 = w_transpose(1)
        regroup("v", w_grp_f32, 1, wt1)
        x_transpose(0, 0)
        x_exit("s", 0, 0)
        quant(w_codes, w_scl, w_grp, 0, 2)
        quant(w_codes, w_scl, w_grp, 2, 4)
        x_quant(0, 0, 2)
        wt2 = w_transpose(2)
        regroup("s", w_grp_f32, 2, wt2)
        wt3 = w_transpose(3)
        regroup("v", w_grp_f32, 3, wt3)
        quant(w_codes, w_scl, w_grp, 4, 6)
        quant(w_codes, w_scl, w_grp, 6, 8)
        x_transpose(0, 1)
        x_exit("s", 0, 1)
        x_quant(0, 2, 4)

        def passes(g, h):
            j = GT * g + 2 * h
            if g == 0 and h == 0:
                mm(0, 0)
                mm(1, 0)
                x_transpose(1, 0)
                x_transpose(1, 1)
                mm(0, 1)
                mm(1, 1)
            elif g == 0:
                mm(2, 0)
                mm(3, 0)
                x_transpose(2, 0)
                mm(2, 1)
                mm(3, 1)
                x_transpose(2, 1)
            elif g == 1:
                mm(j)
                mm(j + 1)
                x_transpose(g + 2, h)
            else:
                if g + 2 < NG:
                    x_transpose(g + 2, h)
                mm(j)
                mm(j + 1)

        def scalar_half(g, h):
            if g == 0:
                if h == 0:
                    s_products(0)
                    s_products(1)
                    x_exit("s", 1, 0)
                    x_exit("s", 1, 1)
                else:
                    s_products(2)
                    s_products(3)
                    x_exit("s", 2, 0)
                    x_exit("s", 2, 1)
                return
            for jj in (2 * h, 2 * h + 1):
                s_products(GT * g + jj)
                if jj % 2 == (g == 1) and g + 2 < NG:
                    x_exit("s", g + 2, h)

        def front(g):
            j = GT * g
            passes(g, 0)
            scalar_half(g, 0)
            if g == 0:
                v_c(j)
                v_c(j + 1)
            passes(g, 1)
            scalar_half(g, 1)
            if g >= 2:
                sine(g - 2, 0, GW)

        front(0)
        for g in range(NG - 1):
            j = GT * g
            if g >= 1:
                cast(g - 1)
            if g == 0:
                v_b0(j)
                v_b0(j + 1)
                x_quant(1, 0, GT)
                v_c(j + 2)
                v_u(j)
                v_c(j + 3)
                v_u(j + 1)
                v_b0(j + 2)
                v_b0(j + 3)
                v_u(j + 2)
                v_u(j + 3)
            else:
                v_b0(j)
                v_b1(j)
                v_b0(j + 1)
                v_b1(j + 1)
                add(g)
                v_c(j + 2)
                v_c(j + 3)
                v_b0(j + 2)
                v_b0(j + 3)
                v_u(j + 2)
                v_u(j + 3)
            if g == 0:
                x_quant(2, 0, GT)
            elif g + 2 < NG:
                x_quant(g + 2, 0, 2)
            if g >= 1:
                sub(g - 1, 0, GW)
            if 0 < g < NG - 2:
                x_quant(g + 2, 2, GT)
            front(g + 1)

        g = NG - 1
        j = GT * g
        cast(g - 1)
        v_b0(j)
        v_b1(j)
        v_b0(j + 1)
        v_b1(j + 1)
        add(g)
        v_c(j + 2)
        v_c(j + 3)
        v_b0(j + 2)
        v_b0(j + 3)
        v_u(j + 2)
        v_u(j + 3)
        sub(g - 1, 0, 2 * C)
        sine(g - 1, 0, 2 * C)
        sub(g - 1, 2 * C, GW)
        sine(g - 1, 2 * C, GW)
        v_cast(g, 2 * C, GW)
        v_cast(g, 0, 2 * C)
        sub(g, 2 * C, 3 * C)
        sine(g, 2 * C, 3 * C)
        sub(g, 3 * C, GW)
        sine(g, 3 * C, GW)
        sub(g, 0, C)
        sine(g, 0, C)
        sub(g, C, 2 * C)
        sine(g, C, 2 * C)
